import numpy as np
import ml_dtypes


def mxq(x, axis, fmt="e4m3"):
    dtype, down = {"e4m3": (ml_dtypes.float8_e4m3fn, 7), "e5m2": (ml_dtypes.float8_e5m2, 14)}[fmt]
    v = np.moveaxis(np.asarray(x, np.float32).astype(ml_dtypes.bfloat16).astype(np.float64), axis, -1)
    blocks = v.reshape(v.shape[:-1] + (-1, 32))
    amax = np.abs(blocks).max(-1, keepdims=True)
    byte = np.maximum(np.where(amax > 0, np.frexp(amax)[1] - 1 + 127, 0) - down, 1)
    scale = np.exp2(byte - 127.0)
    codes = (blocks / scale).astype(np.float32).astype(dtype).astype(np.float64)
    return np.moveaxis((codes * scale).reshape(v.shape), -1, axis)


WIDE = False


def mx_kscale(k):
    if not WIDE:
        return np.ones(k)
    levels = np.array([10, -10, 5, -5, 0])
    if k % 512:
        return np.exp2(np.random.permutation(np.resize(levels, k // 32))).repeat(32)
    a = np.empty((k // 512, 16))
    for p in range(k // 512):
        a[p, :8] = np.random.permutation(np.resize(levels, 8))
        for g in range(8):
            far = levels[np.abs(levels - a[p, g]) >= 10]
            a[p, g + 8] = far[np.random.randint(len(far))]
    return np.exp2(a.ravel()).repeat(32)


BF16 = ml_dtypes.bfloat16


def bf(x):
    return np.asarray(x, np.float32).astype(BF16)


def f64(x):
    return np.asarray(x).astype(np.float64)


B, S, L, H = 2, 16, 8, 512
F = 2 * H
VERT = np.array([[-1, -1, -1], [-1, -1, 1], [-1, 1, -1], [-1, 1, 1], [1, -1, -1], [1, -1, 1], [1, 1, -1], [1, 1, 1]], np.float64) * (np.pi / 2)


def sigmoid(v):
    return 1.0 / (1.0 + np.exp(-v))


def routing_matrix(p, t):
    mid = (p[:, None, :] + p[None, :, :]) * 0.5
    cx, cy, cz = mid[..., 0], mid[..., 1], mid[..., 2]
    f = (np.sin(cx) * np.cos(cy) + np.sin(cy) * np.cos(cz) + np.sin(cz) * np.cos(cx)) - t
    r = sigmoid(2.0 * f)
    r = np.where(np.eye(L) > 0, 1.0, r)
    return r / (r.sum(axis=1, keepdims=True) + 1e-6)


def setup_inputs():
    s = mx_kscale(H)
    return {"x": bf(np.random.standard_normal((B, S, L, H)) * s),
            "limb_positions": bf(VERT + 0.2 * np.random.standard_normal(VERT.shape)),
            "channel_threshold": bf(np.atleast_1d(0.3 + 0.1 * np.random.standard_normal())),
            "W_route": bf(np.random.standard_normal((H, H)) * 2.0 / np.sqrt(H) * s[:, None] / s[None, :]),
            "b_route": bf(np.random.standard_normal(H) * 0.5 * s),
            "W_gate": bf(np.random.standard_normal((H, F)) / np.sqrt(H) / np.concatenate([s, s])[None, :]),
            "b_gate": bf(np.random.standard_normal(H) * 0.5)}


def reference(x, limb_positions, channel_threshold, W_route, b_route, W_gate, b_gate):
    x = f64(x)
    routing = routing_matrix(f64(limb_positions), f64(channel_threshold))
    xq = mxq(x, 3, "e4m3")
    projected = (xq @ mxq(f64(W_route), 1, "e4m3").T) + f64(b_route)
    routed = sum(routing[:, j][None, None, :, None] * projected[:, :, j:j + 1, :] for j in range(L))
    gate_in = np.concatenate([xq, mxq(routed, 3, "e4m3")], axis=-1)
    gate = sigmoid((gate_in @ mxq(f64(W_gate), 1, "e4m3").T) + f64(b_gate))
    return gate * routed + (1.0 - gate) * x

@@ -1,0 +1,354 @@
+import math
+from contextlib import ExitStack
+
+import concourse.mybir as mybir
+from concourse.masks import make_identity
+
+F32 = mybir.dt.float32
+BF16 = mybir.dt.bfloat16
+U32 = mybir.dt.uint32
+U8 = mybir.dt.uint8
+FP8X4 = mybir.dt.float8_e4m3fn_x4
+ALU = mybir.AluOpType
+ACT = mybir.ActivationFunctionType
+AXIS_X = mybir.AxisListType.X
+
+P = 128
+TOKENS = 256
+TOKEN_TILES = TOKENS // P
+LIMBS = 8
+GROUPS = P // LIMBS
+COORDS = 3
+H = 512
+SLOTS = 4
+BANK = 512
+HALF = BANK // 2
+ROUND_MAGIC = 1.5 * 2.0**23
+
+FLOPS = 2 * TOKENS * H * H + 2 * TOKENS * 2 * H * H + 2 * TOKENS * LIMBS * H
+
+
+def transpose_and_group(nc, psum, ident, row_blocks, grouped, on_scalar):
+    bank = psum.tile([P, 2, HALF], F32, tag="bank", name="words_t")
+    for b, rows in enumerate(row_blocks):
+        words = rows.bitcast(F32)
+        for u in range(2):
+            nc.tensor.transpose(bank[:, u, b * P : (b + 1) * P], words[:, u : 2 * P : 2], ident)
+    interleaved = bank[:].rearrange("q u c -> q c u")
+    if on_scalar:
+        nc.scalar.copy(out=grouped.bitcast(F32), in_=interleaved)
+    else:
+        nc.vector.tensor_copy(out=grouped.bitcast(F32), in_=interleaved)
+
+
+def quantise(nc, grouped, codes, scales):
+    nc.vector.quantize_mx(out=codes.bitcast(FP8X4), scales=scales, in_=grouped.rearrange("q c s -> q (c s)"))
+
+
+def tile_tpmslimbrouter_pa_s_kernel(
+    tc, x, limb_positions, channel_threshold, W_route, b_route, W_gate, b_gate, out
+):
+    nc = tc.nc
+    x_rows = x.flatten_outer_dims()
+    out_rows = out.flatten_outer_dims()
+
+    with ExitStack() as ctx:
+        keep = ctx.enter_context(tc.tile_pool(name="keep", bufs=1))
+        psum = ctx.enter_context(tc.psum_pool(name="psum", bufs=8))
+        ctx.enter_context(tc.manual_schedule())
+
+        small_col = keep.tile([P, 1], BF16, name="small_col")
+        nc.gpsimd.memset(small_col[:], 0.0)
+        ident = keep.tile([P, P], F32, name="ident")
+        make_identity(nc, ident[:])
+        warm = keep.tile([P, 1], F32, name="warm")
+        nc.vector.memset(warm[:], 0.0)
+
+        N_POS = LIMBS * COORDS
+        pos_flat = limb_positions.rearrange("i c -> (i c)").unsqueeze(1)
+        nc.sync.dma_start(out=small_col[0:16, :], in_=pos_flat[0:16, :])
+        nc.sync.dma_start(out=small_col[16:N_POS, :], in_=pos_flat[16:N_POS, :])
+        nc.sync.dma_start(out=small_col[N_POS : N_POS + 1, :], in_=channel_threshold.unsqueeze(1))
+        b_route_bf = keep.tile([P, SLOTS], BF16, name="b_route_bf")
+        nc.scalar.dma_start(out=b_route_bf[:], in_=b_route.rearrange("(q s) -> q s", s=SLOTS))
+        b_gate_bf = keep.tile([P, SLOTS], BF16, name="b_gate_bf")
+        nc.scalar.dma_start(out=b_gate_bf[:], in_=b_gate.rearrange("(q s) -> q s", s=SLOTS))
+
+        x_sb = keep.tile([P, TOKEN_TILES, H], BF16, name="x_sb")
+        nc.sync.dma_start(out=x_sb[:], in_=x_rows.rearrange("(n p) k -> p n k", p=P))
+        wr_sb = keep.tile([P, SLOTS, H], BF16, name="wr_sb")
+        wg_sb = keep.tile([P, SLOTS, 2 * H], BF16, name="wg_sb")
+        for w_sb, w in ((wr_sb, W_route), (wg_sb, W_gate)):
+            for u in range(2):
+                nc.sync.dma_start(
+                    out=w_sb[:, 2 * u : 2 * u + 2, :],
+                    in_=w.rearrange("(q s) k -> q s k", s=SLOTS)[:, 2 * u : 2 * u + 2, :],
+                )
+
+        nc.scalar.activation(out=warm[:], in_=warm[:], func=ACT.Silu)
+
+        own_limb = keep.tile([P, LIMBS], F32, name="own_limb")
+        nc.vector.tensor_reduce(
+            out=own_limb[:], in_=ident[:].rearrange("p (a j) -> p j a", j=LIMBS), axis=AXIS_X, op=ALU.add
+        )
+        own_group = keep.tile([P, GROUPS], F32, name="own_group")
+        nc.vector.tensor_reduce(
+            out=own_group[:], in_=ident[:].rearrange("p (a j) -> p a j", j=LIMBS), axis=AXIS_X, op=ALU.add
+        )
+        PAIRS = 1 + LIMBS
+        diag_flat = keep.tile([P, LIMBS * (PAIRS + 1)], F32, name="diag_flat")
+        nc.vector.memset(diag_flat[:], 0.0)
+        nc.vector.memset(diag_flat[:].rearrange("p (i s) -> p i s", s=PAIRS + 1)[:, :, 1], 2.0)
+        two_on_diag = diag_flat[:, 0 : LIMBS * PAIRS].rearrange("p (i s) -> p i s", s=PAIRS)
+        nc.vector.tensor_scalar(out=two_on_diag[:, :, 0], in0=own_limb[:], scalar1=2.0, scalar2=None, op0=ALU.mult)
+        twice_r = keep.tile([P, LIMBS, PAIRS + 1], F32, name="twice_r")
+        nc.vector.memset(twice_r[:, :, PAIRS], 2.0e-6)
+
+        PLANES = 2 * COORDS
+        THR = PLANES * LIMBS
+        comb = keep.tile([P, 64], BF16, name="comb")
+        nc.vector.memset(comb[:], 0.0)
+        unit = ident[:, 0:N_POS].rearrange("k (i c) -> k c i", c=COORDS)
+        planes = comb[:, 0:THR].rearrange("k (g c i) -> k g c i", g=2, c=COORDS)
+        for g, op in enumerate((ALU.add, ALU.subtract)):
+            nc.vector.tensor_tensor(out=planes[:, g, 0:2, :], in0=unit[:, 0:2, :], in1=unit[:, 1:3, :], op=op)
+            nc.vector.tensor_tensor(out=planes[:, g, 2, :], in0=unit[:, 2, :], in1=unit[:, 0, :], op=op)
+        nc.vector.tensor_copy(out=comb[:, THR : THR + 1], in_=ident[:, N_POS : N_POS + 1])
+        combos = psum.tile([P, BANK], F32, tag="bank", name="combos")
+        nc.tensor.matmul(
+            out=combos[:, 0:64], lhsT=small_col[:, 0:1].to_broadcast([P, P]), rhs=comb[:], start=True, stop=True
+        )
+        turns = keep.tile([P, PLANES, LIMBS], F32, name="turns")
+        nc.vector.tensor_scalar(
+            out=turns[:].rearrange("p w i -> p (w i)"),
+            in0=combos[:, 0:THR],
+            scalar1=1.0 / (4.0 * math.pi),
+            scalar2=None,
+            op0=ALU.mult,
+        )
+        minus_thr = keep.tile([P, 1], F32, name="minus_thr")
+        nc.vector.tensor_scalar(
+            out=minus_thr[:], in0=combos[:, THR : THR + 1], scalar1=-1.0, scalar2=None, op0=ALU.mult
+        )
+        pair_shape = [P, PLANES, LIMBS, LIMBS]
+        mid = keep.tile(pair_shape, F32, name="mid")
+        nc.vector.tensor_tensor(
+            out=mid[:],
+            in0=turns[:].unsqueeze(3).to_broadcast(pair_shape),
+            in1=turns[:].unsqueeze(2).to_broadcast(pair_shape),
+            op=ALU.add,
+        )
+        whole = keep.tile(pair_shape, F32, name="whole")
+        nc.vector.tensor_scalar(
+            out=whole[:], in0=mid[:], scalar1=ROUND_MAGIC, scalar2=ROUND_MAGIC, op0=ALU.add, op1=ALU.subtract
+        )
+        frac = keep.tile(pair_shape, F32, name="frac")
+        nc.vector.tensor_tensor(out=frac[:], in0=mid[:], in1=whole[:], op=ALU.subtract)
+
+        b_route_f = keep.tile([P, SLOTS], F32, name="b_route_f")
+        nc.gpsimd.tensor_copy(out=b_route_f[:], in_=b_route_bf[:])
+        half_b_gate = keep.tile([P, SLOTS], F32, name="half_b_gate")
+        nc.gpsimd.tensor_scalar(
+            out=half_b_gate[:],
+            in0=b_gate_bf[:],
+            scalar1=0.5,
+            scalar2=0.0,
+            op0=ALU.mult,
+            op1=ALU.add,
+        )
+
+        x_grouped = keep.tile([P, TOKENS, SLOTS], BF16, name="x_grouped", align_bytes=64)
+        x_codes = keep.tile([P, TOKENS], U32, name="x_codes", align_bytes=64)
+        x_scales = keep.tile([P, TOKENS], U8, name="x_scales", align_bytes=64)
+        wr_grouped = [keep.tile([P, HALF, SLOTS], BF16, name="wr_grouped%d" % u, align_bytes=64) for u in range(2)]
+        wr_codes = keep.tile([P, H], U32, name="wr_codes", align_bytes=64)
+        wr_scales = keep.tile([P, H], U8, name="wr_scales", align_bytes=64)
+
+        transpose_and_group(nc, psum, ident[:], [x_sb[:, n, :] for n in range(TOKEN_TILES)], x_grouped[:], False)
+        sines = keep.tile([P, PLANES, LIMBS * LIMBS], F32, name="sines")
+        nc.scalar.activation(
+            out=sines[:].rearrange("p w n -> p (w n)"),
+            in_=frac[:].rearrange("p w i j -> p (w i j)"),
+            func=ACT.Sin,
+            scale=2.0 * math.pi,
+        )
+        for u in range(2):
+            transpose_and_group(nc, psum, ident[:], [wr_sb[:, 2 * u + e, :] for e in range(2)], wr_grouped[u][:], True)
+
+        b_route_t = psum.tile([P, SLOTS, P], F32, tag="bank", name="b_route_t")
+        for s in range(SLOTS):
+            nc.tensor.transpose(b_route_t[:, s, :], b_route_f[:, s : s + 1].to_broadcast([P, P]), ident[:])
+        b_route_rows = keep.tile([P, SLOTS, P], F32, name="b_route_rows")
+        nc.scalar.copy(out=b_route_rows[:], in_=b_route_t[:])
+
+        gyroid = keep.tile([P, LIMBS, PAIRS], F32, name="gyroid")
+        nc.vector.tensor_reduce(
+            out=gyroid[:, :, 1:PAIRS],
+            in_=sines[:].rearrange("p w (i j) -> p i j w", j=LIMBS),
+            axis=AXIS_X,
+            op=ALU.add,
+        )
+        quantise(nc, x_grouped[:], x_codes[:], x_scales[:])
+        picked = keep.tile([P, LIMBS, LIMBS], F32, name="picked")
+        nc.vector.tensor_tensor(
+            out=picked[:],
+            in0=gyroid[:, :, 1:PAIRS],
+            in1=own_limb[:].unsqueeze(1).to_broadcast([P, LIMBS, LIMBS]),
+            op=ALU.mult,
+        )
+        quantise(nc, wr_grouped[0][:], wr_codes[:, 0:HALF], wr_scales[:, 0:HALF])
+        nc.vector.tensor_reduce(out=gyroid[:, :, 0], in_=picked[:], axis=AXIS_X, op=ALU.add)
+        tanh_f = keep.tile([P, LIMBS, PAIRS], F32, name="tanh_f")
+        nc.scalar.activation(out=tanh_f[:], in_=gyroid[:], func=ACT.Tanh, scale=0.5, bias=minus_thr[:, 0:1])
+        quantise(nc, wr_grouped[1][:], wr_codes[:, HALF:H], wr_scales[:, HALF:H])
+
+        wg_parts = [(u, g) for u in range(2) for g in range(2)]
+        wg_grouped = {
+            part: keep.tile([P, HALF, SLOTS], BF16, name="wg_grouped%d%d" % part, align_bytes=64) for part in wg_parts
+        }
+        wg_codes = [keep.tile([P, H], U32, name="wg_codes%d" % g, align_bytes=64) for g in range(2)]
+        wg_scales = [keep.tile([P, H], U8, name="wg_scales%d" % g, align_bytes=64) for g in range(2)]
+
+        def group_w_gate(u, g):
+            rows = [wg_sb[:, 2 * u + e, g * H : (g + 1) * H] for e in range(2)]
+            transpose_and_group(nc, psum, ident[:], rows, wg_grouped[(u, g)][:], True)
+
+        for part in wg_parts[0:2]:
+            group_w_gate(*part)
+
+        proj_ps = [psum.tile([P, BANK], F32, tag="bank", name="proj_ps%d" % n) for n in range(TOKEN_TILES)]
+        projected = [keep.tile([P, SLOTS, P], F32, name="projected%d" % n) for n in range(TOKEN_TILES)]
+        for n in range(TOKEN_TILES):
+            tokens = slice(n * P, (n + 1) * P)
+            for u in range(2):
+                cols = slice(u * HALF, (u + 1) * HALF)
+                nc.tensor.matmul_mx(
+                    out=proj_ps[n][:, cols],
+                    lhsT=x_codes[:, tokens].bitcast(FP8X4),
+                    lhsT_scale=x_scales[:, tokens],
+                    rhs=wr_codes[:, cols].bitcast(FP8X4),
+                    rhs_scale=wr_scales[:, cols],
+                    start=True,
+                    stop=True,
+                )
+
+        def add_b_route(n, u):
+            cols = slice(u * HALF, (u + 1) * HALF)
+            nc.vector.tensor_tensor(
+                out=projected[n][:].rearrange("t s q -> t (s q)")[:, cols],
+                in0=proj_ps[n][:, cols],
+                in1=b_route_rows[:].rearrange("t s q -> t (s q)")[:, cols],
+                op=ALU.add,
+            )
+
+        nc.vector.scalar_tensor_tensor(
+            out=twice_r[:, :, 0:PAIRS], in0=tanh_f[:], scalar=1.0, in1=two_on_diag, op0=ALU.add, op1=ALU.max
+        )
+        add_b_route(0, 0)
+        row_sum = keep.tile([P, LIMBS], F32, name="row_sum")
+        nc.vector.tensor_reduce(out=row_sum[:], in_=twice_r[:, :, 1 : PAIRS + 1], axis=AXIS_X, op=ALU.add)
+        add_b_route(0, 1)
+        row_inv = keep.tile([P, LIMBS], F32, name="row_inv")
+        nc.vector.reciprocal(out=row_inv[:], in_=row_sum[:])
+        to_limb = keep.tile([P, LIMBS], F32, name="to_limb")
+        nc.vector.tensor_tensor(out=to_limb[:], in0=twice_r[:, :, 0], in1=row_inv[:], op=ALU.mult)
+        mixer = keep.tile([P, GROUPS, LIMBS], F32, name="mixer")
+        nc.vector.tensor_tensor(
+            out=mixer[:],
+            in0=own_group[:].unsqueeze(2).to_broadcast([P, GROUPS, LIMBS]),
+            in1=to_limb[:].unsqueeze(1).to_broadcast([P, GROUPS, LIMBS]),
+            op=ALU.mult,
+        )
+        for u in range(2):
+            add_b_route(1, u)
+
+        for part in wg_parts[2:4]:
+            group_w_gate(*part)
+        for u, g in wg_parts:
+            cols = slice(u * HALF, (u + 1) * HALF)
+            quantise(nc, wg_grouped[(u, g)][:], wg_codes[g][:, cols], wg_scales[g][:, cols])
+
+        r_codes = keep.tile([P, TOKENS], U32, name="r_codes", align_bytes=64)
+        r_scales = keep.tile([P, TOKENS], U8, name="r_scales", align_bytes=64)
+        diff = [keep.tile([P, SLOTS, P], F32, name="diff%d" % n) for n in range(TOKEN_TILES)]
+        for n in range(TOKEN_TILES):
+            tokens = slice(n * P, (n + 1) * P)
+            routed_ps = psum.tile([P, SLOTS, P], F32, tag="bank", name="routed_ps")
+            for s in range(SLOTS):
+                nc.tensor.matmul(
+                    out=routed_ps[:, s, :],
+                    lhsT=projected[n][:, s, :],
+                    rhs=mixer[:].rearrange("t a i -> t (a i)"),
+                    start=True,
+                    stop=True,
+                )
+            r_grouped = keep.tile([P, P, SLOTS], BF16, name="r_grouped%d" % n, align_bytes=64)
+            nc.scalar.copy(out=r_grouped[:], in_=routed_ps[:].rearrange("q s t -> q t s"))
+            quantise(nc, r_grouped[:], r_codes[:, tokens], r_scales[:, tokens])
+            nc.vector.tensor_tensor(
+                out=diff[n][:],
+                in0=routed_ps[:],
+                in1=x_grouped[:, tokens, :].rearrange("q t s -> q s t"),
+                op=ALU.subtract,
+            )
+
+        units = [(n, u) for n in range(TOKEN_TILES) for u in range(2)]
+        tanh_g = {unit: keep.tile([P, 2, P], F32, name="tanh_g%d%d" % unit) for unit in units}
+        for n, u in units:
+            tokens = slice(n * P, (n + 1) * P)
+            gate_ps = psum.tile([P, 2, P], F32, tag="bank", name="gate_ps")
+            for e in range(2):
+                feats = slice((2 * u + e) * P, (2 * u + e + 1) * P)
+                for g, (codes, scales) in enumerate(((x_codes, x_scales), (r_codes, r_scales))):
+                    nc.tensor.matmul_mx(
+                        out=gate_ps[:, e, :],
+                        lhsT=wg_codes[g][:, feats].bitcast(FP8X4),
+                        lhsT_scale=wg_scales[g][:, feats],
+                        rhs=codes[:, tokens].bitcast(FP8X4),
+                        rhs_scale=scales[:, tokens],
+                        start=(g == 0),
+                        stop=(g == 1),
+                    )
+            for e in range(2):
+                nc.scalar.activation(
+                    out=tanh_g[(n, u)][:, e, :],
+                    in_=gate_ps[:, e, :],
+                    func=ACT.Tanh,
+                    scale=0.5,
+                    bias=half_b_gate[:, 2 * u + e : 2 * u + e + 1],
+                )
+
+        moved_t = {}
+
+        def weigh_and_transpose(n, u):
+            moved = keep.tile([P, 2, P], F32, name="moved%d%d" % (n, u))
+            nc.vector.scalar_tensor_tensor(
+                out=moved[:].rearrange("q e t -> q (e t)"),
+                in0=tanh_g[(n, u)][:].rearrange("q e t -> q (e t)"),
+                scalar=1.0,
+                in1=diff[n][:, 2 * u : 2 * u + 2, :].rearrange("q e t -> q (e t)"),
+                op0=ALU.add,
+                op1=ALU.mult,
+            )
+            if u == 0:
+                moved_t[n] = psum.tile([P, SLOTS, P], F32, tag="bank", name="moved_t")
+            for e in range(2):
+                nc.tensor.transpose(moved_t[n][:, 2 * u + e, :], moved[:, e, :], ident[:])
+
+        def add_x_and_store(n, h):
+            feats = slice(h * HALF, (h + 1) * HALF)
+            out_sb = keep.tile([P, HALF], F32, name="out_sb%d%d" % (n, h))
+            nc.vector.scalar_tensor_tensor(
+                out=out_sb[:].rearrange("t (q s) -> t q s", s=SLOTS),
+                in0=moved_t[n][:, :, h * (P // 2) : (h + 1) * (P // 2)].rearrange("t s q -> t q s"),
+                scalar=0.5,
+                in1=x_sb[:, n, feats].rearrange("t (q s) -> t q s", s=SLOTS),
+                op0=ALU.mult,
+                op1=ALU.add,
+            )
+            nc.sync.dma_start(out=out_rows[n * P : (n + 1) * P, feats], in_=out_sb[:])
+
+        for unit in units:
+            weigh_and_transpose(*unit)
+        for unit in units:
+            add_x_and_store(*unit)

@@ -28,17 +28,15 @@ ROUND_MAGIC = 1.5 * 2.0**23
 FLOPS = 2 * TOKENS * H * H + 2 * TOKENS * 2 * H * H + 2 * TOKENS * LIMBS * H
 
 
-def transpose_and_group(nc, psum, ident, row_blocks, grouped, on_scalar):
-    bank = psum.tile([P, 2, HALF], F32, tag="bank", name="words_t")
+def transpose_words(nc, bank, ident, row_blocks):
     for b, rows in enumerate(row_blocks):
         words = rows.bitcast(F32)
         for u in range(2):
             nc.tensor.transpose(bank[:, u, b * P : (b + 1) * P], words[:, u : 2 * P : 2], ident)
-    interleaved = bank[:].rearrange("q u c -> q c u")
-    if on_scalar:
-        nc.scalar.copy(out=grouped.bitcast(F32), in_=interleaved)
-    else:
-        nc.vector.tensor_copy(out=grouped.bitcast(F32), in_=interleaved)
+
+
+def group_words(copy, bank, grouped):
+    copy(out=grouped.bitcast(F32), in_=bank.rearrange("q u c -> q c u"))
 
 
 def quantise(nc, grouped, codes, scales):
@@ -64,18 +62,17 @@ def tile_tpmslimbrouter_pa_s_kernel(
         warm = keep.tile([P, 1], F32, name="warm")
         nc.vector.memset(warm[:], 0.0)
 
+        x_sb = keep.tile([P, TOKEN_TILES, H], BF16, name="x_sb")
+        nc.sync.dma_start(out=x_sb[:], in_=x_rows.rearrange("(n p) k -> p n k", p=P))
         N_POS = LIMBS * COORDS
         pos_flat = limb_positions.rearrange("i c -> (i c)").unsqueeze(1)
         nc.sync.dma_start(out=small_col[0:16, :], in_=pos_flat[0:16, :])
         nc.sync.dma_start(out=small_col[16:N_POS, :], in_=pos_flat[16:N_POS, :])
-        nc.sync.dma_start(out=small_col[N_POS : N_POS + 1, :], in_=channel_threshold.unsqueeze(1))
+        thr_bf = keep.tile([P, 1], BF16, name="thr_bf")
+        nc.scalar.dma_start(out=thr_bf[:], in_=channel_threshold.partition_broadcast(P))
         b_route_bf = keep.tile([P, SLOTS], BF16, name="b_route_bf")
         nc.scalar.dma_start(out=b_route_bf[:], in_=b_route.rearrange("(q s) -> q s", s=SLOTS))
-        b_gate_bf = keep.tile([P, SLOTS], BF16, name="b_gate_bf")
-        nc.scalar.dma_start(out=b_gate_bf[:], in_=b_gate.rearrange("(q s) -> q s", s=SLOTS))
 
-        x_sb = keep.tile([P, TOKEN_TILES, H], BF16, name="x_sb")
-        nc.sync.dma_start(out=x_sb[:], in_=x_rows.rearrange("(n p) k -> p n k", p=P))
         wr_sb = keep.tile([P, SLOTS, H], BF16, name="wr_sb")
         wg_sb = keep.tile([P, SLOTS, 2 * H], BF16, name="wg_sb")
         for w_sb, w in ((wr_sb, W_route), (wg_sb, W_gate)):
@@ -84,6 +81,9 @@ def tile_tpmslimbrouter_pa_s_kernel(
                     out=w_sb[:, 2 * u : 2 * u + 2, :],
                     in_=w.rearrange("(q s) k -> q s k", s=SLOTS)[:, 2 * u : 2 * u + 2, :],
                 )
+
+        b_gate_bf = keep.tile([P, SLOTS], BF16, name="b_gate_bf")
+        nc.sync.dma_start(out=b_gate_bf[:], in_=b_gate.rearrange("(q s) -> q s", s=SLOTS))
 
         nc.scalar.activation(out=warm[:], in_=warm[:], func=ACT.Silu)
 
@@ -95,163 +95,171 @@ def tile_tpmslimbrouter_pa_s_kernel(
         nc.vector.tensor_reduce(
             out=own_group[:], in_=ident[:].rearrange("p (a j) -> p a j", j=LIMBS), axis=AXIS_X, op=ALU.add
         )
-        PAIRS = 1 + LIMBS
-        diag_flat = keep.tile([P, LIMBS * (PAIRS + 1)], F32, name="diag_flat")
-        nc.vector.memset(diag_flat[:], 0.0)
-        nc.vector.memset(diag_flat[:].rearrange("p (i s) -> p i s", s=PAIRS + 1)[:, :, 1], 2.0)
-        two_on_diag = diag_flat[:, 0 : LIMBS * PAIRS].rearrange("p (i s) -> p i s", s=PAIRS)
-        nc.vector.tensor_scalar(out=two_on_diag[:, :, 0], in0=own_limb[:], scalar1=2.0, scalar2=None, op0=ALU.mult)
-        twice_r = keep.tile([P, LIMBS, PAIRS + 1], F32, name="twice_r")
-        nc.vector.memset(twice_r[:, :, PAIRS], 2.0e-6)
+        two_on_diag = keep.tile([P, LIMBS], F32, name="two_on_diag")
+        nc.vector.tensor_scalar(out=two_on_diag[:], in0=own_limb[:], scalar1=2.0, scalar2=None, op0=ALU.mult)
+        coord_of = keep.tile([P, LIMBS], F32, name="coord_of")
+        nc.vector.tensor_reduce(
+            out=coord_of[:], in_=ident[:, 0:N_POS].rearrange("k (i c) -> k i c", c=COORDS), axis=AXIS_X, op=ALU.add
+        )
+        sixteenth = keep.tile([P, 1], F32, name="sixteenth")
+        nc.vector.memset(sixteenth[:], 1.0 / GROUPS)
+        eps = keep.tile([P, LIMBS], F32, name="eps")
+        nc.vector.tensor_scalar(
+            out=eps[:], in0=own_limb[:], scalar1=0.0, scalar2=2.0e-6 * GROUPS / P, op0=ALU.mult, op1=ALU.add
+        )
 
         PLANES = 2 * COORDS
-        THR = PLANES * LIMBS
-        comb = keep.tile([P, 64], BF16, name="comb")
-        nc.vector.memset(comb[:], 0.0)
+        WIDTH = PLANES * LIMBS
         unit = ident[:, 0:N_POS].rearrange("k (i c) -> k c i", c=COORDS)
-        planes = comb[:, 0:THR].rearrange("k (g c i) -> k g c i", g=2, c=COORDS)
+        of_limb = keep.tile([P, WIDTH], BF16, name="of_limb")
+        planes = of_limb[:].rearrange("k (g c i) -> k g c i", g=2, c=COORDS)
         for g, op in enumerate((ALU.add, ALU.subtract)):
             nc.vector.tensor_tensor(out=planes[:, g, 0:2, :], in0=unit[:, 0:2, :], in1=unit[:, 1:3, :], op=op)
             nc.vector.tensor_tensor(out=planes[:, g, 2, :], in0=unit[:, 2, :], in1=unit[:, 0, :], op=op)
-        nc.vector.tensor_copy(out=comb[:, THR : THR + 1], in_=ident[:, N_POS : N_POS + 1])
-        combos = psum.tile([P, BANK], F32, tag="bank", name="combos")
-        nc.tensor.matmul(
-            out=combos[:, 0:64], lhsT=small_col[:, 0:1].to_broadcast([P, P]), rhs=comb[:], start=True, stop=True
+        own_planes = keep.tile([P, PLANES], F32, name="own_planes")
+        nc.vector.tensor_reduce(
+            out=own_planes[:], in_=of_limb[:].rearrange("k (w i) -> k w i", i=LIMBS), axis=AXIS_X, op=ALU.add
         )
-        turns = keep.tile([P, PLANES, LIMBS], F32, name="turns")
+        of_own = keep.tile([P, WIDTH], BF16, name="of_own")
+        nc.vector.tensor_copy(
+            out=of_own[:].rearrange("k (w i) -> k w i", i=LIMBS),
+            in_=own_planes[:].unsqueeze(2).to_broadcast([P, PLANES, LIMBS]),
+        )
+        small_own = keep.tile([P, GROUPS, LIMBS], BF16, name="small_own")
         nc.vector.tensor_scalar(
-            out=turns[:].rearrange("p w i -> p (w i)"),
-            in0=combos[:, 0:THR],
-            scalar1=1.0 / (4.0 * math.pi),
+            out=small_own[:],
+            in0=coord_of[:].unsqueeze(1).to_broadcast([P, GROUPS, LIMBS]),
+            scalar1=small_col[:, 0:1],
             scalar2=None,
             op0=ALU.mult,
         )
         minus_thr = keep.tile([P, 1], F32, name="minus_thr")
-        nc.vector.tensor_scalar(
-            out=minus_thr[:], in0=combos[:, THR : THR + 1], scalar1=-1.0, scalar2=None, op0=ALU.mult
-        )
-        pair_shape = [P, PLANES, LIMBS, LIMBS]
-        mid = keep.tile(pair_shape, F32, name="mid")
-        nc.vector.tensor_tensor(
-            out=mid[:],
-            in0=turns[:].unsqueeze(3).to_broadcast(pair_shape),
-            in1=turns[:].unsqueeze(2).to_broadcast(pair_shape),
-            op=ALU.add,
-        )
-        whole = keep.tile(pair_shape, F32, name="whole")
-        nc.vector.tensor_scalar(
-            out=whole[:], in0=mid[:], scalar1=ROUND_MAGIC, scalar2=ROUND_MAGIC, op0=ALU.add, op1=ALU.subtract
-        )
-        frac = keep.tile(pair_shape, F32, name="frac")
-        nc.vector.tensor_tensor(out=frac[:], in0=mid[:], in1=whole[:], op=ALU.subtract)
+        nc.vector.tensor_scalar(out=minus_thr[:], in0=thr_bf[:], scalar1=-1.0, scalar2=None, op0=ALU.mult)
 
-        b_route_f = keep.tile([P, SLOTS], F32, name="b_route_f")
-        nc.gpsimd.tensor_copy(out=b_route_f[:], in_=b_route_bf[:])
+        ident_bf = keep.tile([P, P], BF16, name="ident_bf")
+        nc.gpsimd.tensor_copy(out=ident_bf[:], in_=ident[:])
         half_b_gate = keep.tile([P, SLOTS], F32, name="half_b_gate")
         nc.gpsimd.tensor_scalar(
-            out=half_b_gate[:],
-            in0=b_gate_bf[:],
-            scalar1=0.5,
-            scalar2=0.0,
-            op0=ALU.mult,
-            op1=ALU.add,
+            out=half_b_gate[:], in0=b_gate_bf[:], scalar1=0.5, scalar2=0.0, op0=ALU.mult, op1=ALU.add
         )
 
         x_grouped = keep.tile([P, TOKENS, SLOTS], BF16, name="x_grouped", align_bytes=64)
         x_codes = keep.tile([P, TOKENS], U32, name="x_codes", align_bytes=64)
         x_scales = keep.tile([P, TOKENS], U8, name="x_scales", align_bytes=64)
-        wr_grouped = [keep.tile([P, HALF, SLOTS], BF16, name="wr_grouped%d" % u, align_bytes=64) for u in range(2)]
+        wr_grouped = [keep.tile([P, P, SLOTS], BF16, name="wr_grouped%d" % s, align_bytes=64) for s in range(SLOTS)]
         wr_codes = keep.tile([P, H], U32, name="wr_codes", align_bytes=64)
         wr_scales = keep.tile([P, H], U8, name="wr_scales", align_bytes=64)
-
-        transpose_and_group(nc, psum, ident[:], [x_sb[:, n, :] for n in range(TOKEN_TILES)], x_grouped[:], False)
-        sines = keep.tile([P, PLANES, LIMBS * LIMBS], F32, name="sines")
-        nc.scalar.activation(
-            out=sines[:].rearrange("p w n -> p (w n)"),
-            in_=frac[:].rearrange("p w i j -> p (w i j)"),
-            func=ACT.Sin,
-            scale=2.0 * math.pi,
-        )
-        for u in range(2):
-            transpose_and_group(nc, psum, ident[:], [wr_sb[:, 2 * u + e, :] for e in range(2)], wr_grouped[u][:], True)
-
-        b_route_t = psum.tile([P, SLOTS, P], F32, tag="bank", name="b_route_t")
-        for s in range(SLOTS):
-            nc.tensor.transpose(b_route_t[:, s, :], b_route_f[:, s : s + 1].to_broadcast([P, P]), ident[:])
-        b_route_rows = keep.tile([P, SLOTS, P], F32, name="b_route_rows")
-        nc.scalar.copy(out=b_route_rows[:], in_=b_route_t[:])
-
-        gyroid = keep.tile([P, LIMBS, PAIRS], F32, name="gyroid")
-        nc.vector.tensor_reduce(
-            out=gyroid[:, :, 1:PAIRS],
-            in_=sines[:].rearrange("p w (i j) -> p i j w", j=LIMBS),
-            axis=AXIS_X,
-            op=ALU.add,
-        )
-        quantise(nc, x_grouped[:], x_codes[:], x_scales[:])
-        picked = keep.tile([P, LIMBS, LIMBS], F32, name="picked")
-        nc.vector.tensor_tensor(
-            out=picked[:],
-            in0=gyroid[:, :, 1:PAIRS],
-            in1=own_limb[:].unsqueeze(1).to_broadcast([P, LIMBS, LIMBS]),
-            op=ALU.mult,
-        )
-        quantise(nc, wr_grouped[0][:], wr_codes[:, 0:HALF], wr_scales[:, 0:HALF])
-        nc.vector.tensor_reduce(out=gyroid[:, :, 0], in_=picked[:], axis=AXIS_X, op=ALU.add)
-        tanh_f = keep.tile([P, LIMBS, PAIRS], F32, name="tanh_f")
-        nc.scalar.activation(out=tanh_f[:], in_=gyroid[:], func=ACT.Tanh, scale=0.5, bias=minus_thr[:, 0:1])
-        quantise(nc, wr_grouped[1][:], wr_codes[:, HALF:H], wr_scales[:, HALF:H])
-
         wg_parts = [(u, g) for u in range(2) for g in range(2)]
         wg_grouped = {
             part: keep.tile([P, HALF, SLOTS], BF16, name="wg_grouped%d%d" % part, align_bytes=64) for part in wg_parts
         }
         wg_codes = [keep.tile([P, H], U32, name="wg_codes%d" % g, align_bytes=64) for g in range(2)]
         wg_scales = [keep.tile([P, H], U8, name="wg_scales%d" % g, align_bytes=64) for g in range(2)]
-
-        def group_w_gate(u, g):
-            rows = [wg_sb[:, 2 * u + e, g * H : (g + 1) * H] for e in range(2)]
-            transpose_and_group(nc, psum, ident[:], rows, wg_grouped[(u, g)][:], True)
-
-        for part in wg_parts[0:2]:
-            group_w_gate(*part)
-
-        proj_ps = [psum.tile([P, BANK], F32, tag="bank", name="proj_ps%d" % n) for n in range(TOKEN_TILES)]
         projected = [keep.tile([P, SLOTS, P], F32, name="projected%d" % n) for n in range(TOKEN_TILES)]
-        for n in range(TOKEN_TILES):
-            tokens = slice(n * P, (n + 1) * P)
-            for u in range(2):
-                cols = slice(u * HALF, (u + 1) * HALF)
+        r_grouped = [keep.tile([P, P, SLOTS], BF16, name="r_grouped%d" % n, align_bytes=64) for n in range(TOKEN_TILES)]
+        r_codes = keep.tile([P, TOKENS], U32, name="r_codes", align_bytes=64)
+        r_scales = keep.tile([P, TOKENS], U8, name="r_scales", align_bytes=64)
+        diff = [keep.tile([P, SLOTS, P], F32, name="diff%d" % n) for n in range(TOKEN_TILES)]
+
+        def tokens_of(n):
+            return slice(n * P, (n + 1) * P)
+
+        def half_cols(u):
+            return slice(u * HALF, (u + 1) * HALF)
+
+        x_words = psum.tile([P, 2, HALF], F32, tag="bank", name="x_words")
+        transpose_words(nc, x_words, ident[:], [x_sb[:, n, :] for n in range(TOKEN_TILES)])
+        wr_words = [psum.tile([P, 2, P], F32, tag="bank", name="wr_words") for s in range(SLOTS)]
+        routing_ps = psum.tile([P, BANK], F32, tag="bank", name="routing_ps")
+        angles = routing_ps[:, 0:WIDTH]
+        sums = routing_ps[:, WIDTH : WIDTH + LIMBS]
+        nc.tensor.matmul(
+            out=angles, lhsT=small_col[:, 0:1].to_broadcast([P, P]), rhs=of_limb[:], start=True, stop=False
+        )
+        nc.tensor.matmul(
+            out=angles, lhsT=small_own[:].rearrange("k a j -> k (a j)"), rhs=of_own[:], start=False, stop=True
+        )
+        group_words(nc.scalar.copy, x_words[:], x_grouped[:])
+        TURN = 1.0 / (4.0 * math.pi)
+        turns = keep.tile([P, WIDTH], F32, name="turns")
+        nc.vector.tensor_scalar(out=turns[:], in0=angles, scalar1=TURN, scalar2=None, op0=ALU.mult)
+        rounded = keep.tile([P, WIDTH], F32, name="rounded")
+        nc.vector.tensor_scalar(
+            out=rounded[:], in0=angles, scalar1=TURN, scalar2=ROUND_MAGIC, op0=ALU.mult, op1=ALU.add
+        )
+        minus_frac = keep.tile([P, WIDTH], F32, name="minus_frac")
+        nc.vector.scalar_tensor_tensor(
+            out=minus_frac[:], in0=rounded[:], scalar=ROUND_MAGIC, in1=turns[:], op0=ALU.subtract, op1=ALU.subtract
+        )
+        for s in range(SLOTS):
+            transpose_words(nc, wr_words[s], ident[:], [wr_sb[:, s, :]])
+
+        def quantise_wr(s):
+            quantise(nc, wr_grouped[s][:], wr_codes[:, s * P : (s + 1) * P], wr_scales[:, s * P : (s + 1) * P])
+
+        group_words(nc.scalar.copy, wr_words[0][:], wr_grouped[0][:])
+        sines = keep.tile([P, WIDTH], F32, name="sines")
+        nc.scalar.activation(out=sines[:], in_=minus_frac[:], func=ACT.Sin, scale=-2.0 * math.pi)
+        quantise(nc, x_grouped[:], x_codes[:], x_scales[:])
+        group_words(nc.vector.tensor_copy, wr_words[1][:], wr_grouped[1][:])
+        group_words(nc.scalar.copy, wr_words[2][:], wr_grouped[2][:])
+        gyroid = keep.tile([P, LIMBS], F32, name="gyroid")
+        nc.vector.tensor_reduce(
+            out=gyroid[:], in_=sines[:].rearrange("p (w i) -> p i w", i=LIMBS), axis=AXIS_X, op=ALU.add
+        )
+        quantise_wr(0)
+        quantise_wr(1)
+        tanh_f = keep.tile([P, LIMBS], F32, name="tanh_f")
+        nc.scalar.activation(out=tanh_f[:], in_=gyroid[:], func=ACT.Tanh, scale=0.5, bias=minus_thr[:, 0:1])
+        group_words(nc.scalar.copy, wr_words[3][:], wr_grouped[3][:])
+        quantise_wr(2)
+        twice_r = keep.tile([P, LIMBS], F32, name="twice_r")
+        nc.vector.scalar_tensor_tensor(
+            out=twice_r[:], in0=tanh_f[:], scalar=1.0, in1=two_on_diag[:], op0=ALU.add, op1=ALU.max
+        )
+        quantise_wr(3)
+
+        b_route_t = psum.tile([P, SLOTS, P], BF16, tag="bank", name="b_route_t")
+        for s in range(SLOTS):
+            nc.tensor.transpose(b_route_t[:, s, :], b_route_bf[:, s : s + 1].to_broadcast([P, P]), ident_bf[:])
+        b_route_rows = keep.tile([P, SLOTS, P], BF16, name="b_route_rows")
+        nc.scalar.copy(out=b_route_rows[:], in_=b_route_t[:])
+
+        def group_w_gate(words, u, g):
+            transpose_words(nc, words, ident[:], [wg_sb[:, 2 * u + e, g * H : (g + 1) * H] for e in range(2)])
+            group_words(nc.scalar.copy, words[:], wg_grouped[(u, g)][:])
+
+        first_words = psum.tile([P, 2, HALF], F32, tag="bank", name="wg_words")
+        group_w_gate(first_words, 0, 0)
+
+        def project(u):
+            for n in range(TOKEN_TILES):
                 nc.tensor.matmul_mx(
-                    out=proj_ps[n][:, cols],
-                    lhsT=x_codes[:, tokens].bitcast(FP8X4),
-                    lhsT_scale=x_scales[:, tokens],
-                    rhs=wr_codes[:, cols].bitcast(FP8X4),
-                    rhs_scale=wr_scales[:, cols],
+                    out=proj_ps[n][:, half_cols(u)],
+                    lhsT=x_codes[:, tokens_of(n)].bitcast(FP8X4),
+                    lhsT_scale=x_scales[:, tokens_of(n)],
+                    rhs=wr_codes[:, half_cols(u)].bitcast(FP8X4),
+                    rhs_scale=wr_scales[:, half_cols(u)],
                     start=True,
                     stop=True,
                 )
 
-        def add_b_route(n, u):
-            cols = slice(u * HALF, (u + 1) * HALF)
-            nc.vector.tensor_tensor(
-                out=projected[n][:].rearrange("t s q -> t (s q)")[:, cols],
-                in0=proj_ps[n][:, cols],
-                in1=b_route_rows[:].rearrange("t s q -> t (s q)")[:, cols],
-                op=ALU.add,
-            )
+        wg_words = [psum.tile([P, 2, HALF], F32, tag="bank", name="wg_words") for part in wg_parts[1:]]
+        proj_ps = [psum.tile([P, BANK], F32, tag="bank", name="proj_ps%d" % n) for n in range(TOKEN_TILES)]
+        group_w_gate(wg_words[0], 0, 1)
+        project(0)
 
-        nc.vector.scalar_tensor_tensor(
-            out=twice_r[:, :, 0:PAIRS], in0=tanh_f[:], scalar=1.0, in1=two_on_diag, op0=ALU.add, op1=ALU.max
-        )
-        add_b_route(0, 0)
-        row_sum = keep.tile([P, LIMBS], F32, name="row_sum")
-        nc.vector.tensor_reduce(out=row_sum[:], in_=twice_r[:, :, 1 : PAIRS + 1], axis=AXIS_X, op=ALU.add)
-        add_b_route(0, 1)
+        sum_all = sixteenth[:, 0:1].to_broadcast([P, P])
+        nc.tensor.matmul(out=sums, lhsT=sum_all, rhs=eps[:], start=True, stop=False)
+        nc.tensor.matmul(out=sums, lhsT=sum_all, rhs=twice_r[:], start=False, stop=True)
         row_inv = keep.tile([P, LIMBS], F32, name="row_inv")
-        nc.vector.reciprocal(out=row_inv[:], in_=row_sum[:])
+        nc.vector.reciprocal(out=row_inv[:], in_=sums)
         to_limb = keep.tile([P, LIMBS], F32, name="to_limb")
-        nc.vector.tensor_tensor(out=to_limb[:], in0=twice_r[:, :, 0], in1=row_inv[:], op=ALU.mult)
+        nc.vector.tensor_tensor(out=to_limb[:], in0=twice_r[:], in1=row_inv[:], op=ALU.mult)
+
+        project(1)
+        group_w_gate(wg_words[1], 1, 0)
+        group_w_gate(wg_words[2], 1, 1)
         mixer = keep.tile([P, GROUPS, LIMBS], F32, name="mixer")
         nc.vector.tensor_tensor(
             out=mixer[:],
@@ -259,96 +267,125 @@ def tile_tpmslimbrouter_pa_s_kernel(
             in1=to_limb[:].unsqueeze(1).to_broadcast([P, GROUPS, LIMBS]),
             op=ALU.mult,
         )
-        for u in range(2):
-            add_b_route(1, u)
-
-        for part in wg_parts[2:4]:
-            group_w_gate(*part)
-        for u, g in wg_parts:
-            cols = slice(u * HALF, (u + 1) * HALF)
-            quantise(nc, wg_grouped[(u, g)][:], wg_codes[g][:, cols], wg_scales[g][:, cols])
-
-        r_codes = keep.tile([P, TOKENS], U32, name="r_codes", align_bytes=64)
-        r_scales = keep.tile([P, TOKENS], U8, name="r_scales", align_bytes=64)
-        diff = [keep.tile([P, SLOTS, P], F32, name="diff%d" % n) for n in range(TOKEN_TILES)]
         for n in range(TOKEN_TILES):
-            tokens = slice(n * P, (n + 1) * P)
-            routed_ps = psum.tile([P, SLOTS, P], F32, tag="bank", name="routed_ps")
+            for u in range(2):
+                nc.vector.tensor_tensor(
+                    out=projected[n][:].rearrange("t s q -> t (s q)")[:, half_cols(u)],
+                    in0=proj_ps[n][:, half_cols(u)],
+                    in1=b_route_rows[:].rearrange("t s q -> t (s q)")[:, half_cols(u)],
+                    op=ALU.add,
+                )
+        routed_ps = [psum.tile([P, SLOTS, P], F32, tag="bank", name="routed_ps%d" % n) for n in range(TOKEN_TILES)]
+
+        def mix(n):
             for s in range(SLOTS):
                 nc.tensor.matmul(
-                    out=routed_ps[:, s, :],
+                    out=routed_ps[n][:, s, :],
                     lhsT=projected[n][:, s, :],
                     rhs=mixer[:].rearrange("t a i -> t (a i)"),
                     start=True,
                     stop=True,
                 )
-            r_grouped = keep.tile([P, P, SLOTS], BF16, name="r_grouped%d" % n, align_bytes=64)
-            nc.scalar.copy(out=r_grouped[:], in_=routed_ps[:].rearrange("q s t -> q t s"))
-            quantise(nc, r_grouped[:], r_codes[:, tokens], r_scales[:, tokens])
+
+        def round_routed(n):
+            nc.scalar.copy(out=r_grouped[n][:], in_=routed_ps[n][:].rearrange("q s t -> q t s"))
+
+        def quantise_routed(n):
+            quantise(nc, r_grouped[n][:], r_codes[:, tokens_of(n)], r_scales[:, tokens_of(n)])
+
+        def subtract_x(n):
             nc.vector.tensor_tensor(
                 out=diff[n][:],
-                in0=routed_ps[:],
-                in1=x_grouped[:, tokens, :].rearrange("q t s -> q s t"),
+                in0=routed_ps[n][:],
+                in1=x_grouped[:, tokens_of(n), :].rearrange("q t s -> q s t"),
                 op=ALU.subtract,
             )
 
-        units = [(n, u) for n in range(TOKEN_TILES) for u in range(2)]
-        tanh_g = {unit: keep.tile([P, 2, P], F32, name="tanh_g%d%d" % unit) for unit in units}
-        for n, u in units:
-            tokens = slice(n * P, (n + 1) * P)
-            gate_ps = psum.tile([P, 2, P], F32, tag="bank", name="gate_ps")
-            for e in range(2):
-                feats = slice((2 * u + e) * P, (2 * u + e + 1) * P)
-                for g, (codes, scales) in enumerate(((x_codes, x_scales), (r_codes, r_scales))):
-                    nc.tensor.matmul_mx(
-                        out=gate_ps[:, e, :],
-                        lhsT=wg_codes[g][:, feats].bitcast(FP8X4),
-                        lhsT_scale=wg_scales[g][:, feats],
-                        rhs=codes[:, tokens].bitcast(FP8X4),
-                        rhs_scale=scales[:, tokens],
-                        start=(g == 0),
-                        stop=(g == 1),
-                    )
-            for e in range(2):
-                nc.scalar.activation(
-                    out=tanh_g[(n, u)][:, e, :],
-                    in_=gate_ps[:, e, :],
-                    func=ACT.Tanh,
-                    scale=0.5,
-                    bias=half_b_gate[:, 2 * u + e : 2 * u + e + 1],
-                )
+        def quantise_w_gate(u, g):
+            quantise(nc, wg_grouped[(u, g)][:], wg_codes[g][:, half_cols(u)], wg_scales[g][:, half_cols(u)])
 
-        moved_t = {}
+        for n in range(TOKEN_TILES):
+            mix(n)
+            round_routed(n)
+        for part in wg_parts:
+            quantise_w_gate(*part)
+        quantise_routed(0)
+        subtract_x(0)
 
-        def weigh_and_transpose(n, u):
-            moved = keep.tile([P, 2, P], F32, name="moved%d%d" % (n, u))
+        def gate_pass(out, n, s, g):
+            feats = slice(s * P, (s + 1) * P)
+            codes, scales = ((x_codes, x_scales), (r_codes, r_scales))[g]
+            nc.tensor.matmul_mx(
+                out=out,
+                lhsT=wg_codes[g][:, feats].bitcast(FP8X4),
+                lhsT_scale=wg_scales[g][:, feats],
+                rhs=codes[:, tokens_of(n)].bitcast(FP8X4),
+                rhs_scale=scales[:, tokens_of(n)],
+                start=(g == 0),
+                stop=(g == 1),
+            )
+
+        tanh_g = [keep.tile([P, SLOTS, P], F32, name="tanh_g%d" % n) for n in range(TOKEN_TILES)]
+
+        def gate(out, n, s):
+            nc.scalar.activation(
+                out=tanh_g[n][:, s, :], in_=out, func=ACT.Tanh, scale=0.5, bias=half_b_gate[:, s : s + 1]
+            )
+
+        gates_0 = [psum.tile([P, 2, P], F32, tag="bank", name="gates_0") for u in range(2)]
+        for s in range(SLOTS):
+            for g in range(2):
+                gate_pass(gates_0[s // 2][:, s % 2, :], 0, s, g)
+        gates_1 = [psum.tile([P, P], F32, tag="bank", name="gates_1") for s in range(SLOTS)]
+        for s in range(SLOTS):
+            gate_pass(gates_1[s][:], 1, s, 0)
+        quantise_routed(1)
+        for s in range(SLOTS):
+            gate_pass(gates_1[s][:], 1, s, 1)
+        for s in range(SLOTS):
+            gate(gates_0[s // 2][:, s % 2, :], 0, s)
+        for s in range(SLOTS):
+            gate(gates_1[s][:], 1, s)
+
+        moved = [keep.tile([P, SLOTS, P], F32, name="moved%d" % n) for n in range(TOKEN_TILES)]
+
+        def weigh(n, u):
+            slots = slice(2 * u, 2 * u + 2)
             nc.vector.scalar_tensor_tensor(
-                out=moved[:].rearrange("q e t -> q (e t)"),
-                in0=tanh_g[(n, u)][:].rearrange("q e t -> q (e t)"),
+                out=moved[n][:, slots, :].rearrange("q e t -> q (e t)"),
+                in0=tanh_g[n][:, slots, :].rearrange("q e t -> q (e t)"),
                 scalar=1.0,
-                in1=diff[n][:, 2 * u : 2 * u + 2, :].rearrange("q e t -> q (e t)"),
+                in1=diff[n][:, slots, :].rearrange("q e t -> q (e t)"),
                 op0=ALU.add,
                 op1=ALU.mult,
             )
-            if u == 0:
-                moved_t[n] = psum.tile([P, SLOTS, P], F32, tag="bank", name="moved_t")
-            for e in range(2):
-                nc.tensor.transpose(moved_t[n][:, 2 * u + e, :], moved[:, e, :], ident[:])
 
-        def add_x_and_store(n, h):
-            feats = slice(h * HALF, (h + 1) * HALF)
+        def transpose_back(moved_t, n, u):
+            for s in (2 * u, 2 * u + 1):
+                nc.tensor.transpose(moved_t[:, s, :], moved[n][:, s, :], ident[:])
+
+        def add_x_and_store(moved_t, n, h):
+            feats = half_cols(h)
             out_sb = keep.tile([P, HALF], F32, name="out_sb%d%d" % (n, h))
             nc.vector.scalar_tensor_tensor(
                 out=out_sb[:].rearrange("t (q s) -> t q s", s=SLOTS),
-                in0=moved_t[n][:, :, h * (P // 2) : (h + 1) * (P // 2)].rearrange("t s q -> t q s"),
+                in0=moved_t[:, :, h * (P // 2) : (h + 1) * (P // 2)].rearrange("t s q -> t q s"),
                 scalar=0.5,
                 in1=x_sb[:, n, feats].rearrange("t (q s) -> t q s", s=SLOTS),
                 op0=ALU.mult,
                 op1=ALU.add,
             )
-            nc.sync.dma_start(out=out_rows[n * P : (n + 1) * P, feats], in_=out_sb[:])
+            nc.sync.dma_start(out=out_rows[tokens_of(n), feats], in_=out_sb[:])
 
-        for unit in units:
-            weigh_and_transpose(*unit)
-        for unit in units:
-            add_x_and_store(*unit)
+        weigh(0, 0)
+        subtract_x(1)
+        moved_t = [psum.tile([P, SLOTS, P], F32, tag="bank", name="moved_t%d" % n) for n in range(TOKEN_TILES)]
+        transpose_back(moved_t[0], 0, 0)
+        weigh(0, 1)
+        transpose_back(moved_t[0], 0, 1)
+        for u in range(2):
+            weigh(1, u)
+            transpose_back(moved_t[1], 1, u)
+        for n in range(TOKEN_TILES):
+            for h in range(2):
+                add_x_and_store(moved_t[n], n, h)

@@ -201,22 +201,22 @@ def tile_tpmslimbrouter_pa_s_kernel(
         sines = keep.tile([P, WIDTH], F32, name="sines")
         nc.scalar.activation(out=sines[:], in_=minus_frac[:], func=ACT.Sin, scale=-2.0 * math.pi)
         quantise(nc, x_grouped[:], x_codes[:], x_scales[:])
-        group_words(nc.vector.tensor_copy, wr_words[1][:], wr_grouped[1][:])
-        group_words(nc.scalar.copy, wr_words[2][:], wr_grouped[2][:])
         gyroid = keep.tile([P, LIMBS], F32, name="gyroid")
         nc.vector.tensor_reduce(
             out=gyroid[:], in_=sines[:].rearrange("p (w i) -> p i w", i=LIMBS), axis=AXIS_X, op=ALU.add
         )
+        group_words(nc.vector.tensor_copy, wr_words[1][:], wr_grouped[1][:])
+        group_words(nc.scalar.copy, wr_words[2][:], wr_grouped[2][:])
         quantise_wr(0)
         quantise_wr(1)
         tanh_f = keep.tile([P, LIMBS], F32, name="tanh_f")
         nc.scalar.activation(out=tanh_f[:], in_=gyroid[:], func=ACT.Tanh, scale=0.5, bias=minus_thr[:, 0:1])
-        group_words(nc.scalar.copy, wr_words[3][:], wr_grouped[3][:])
-        quantise_wr(2)
         twice_r = keep.tile([P, LIMBS], F32, name="twice_r")
         nc.vector.scalar_tensor_tensor(
             out=twice_r[:], in0=tanh_f[:], scalar=1.0, in1=two_on_diag[:], op0=ALU.add, op1=ALU.max
         )
+        group_words(nc.scalar.copy, wr_words[3][:], wr_grouped[3][:])
+        quantise_wr(2)
         quantise_wr(3)
 
         b_route_t = psum.tile([P, SLOTS, P], BF16, tag="bank", name="b_route_t")
@@ -225,12 +225,27 @@ def tile_tpmslimbrouter_pa_s_kernel(
         b_route_rows = keep.tile([P, SLOTS, P], BF16, name="b_route_rows")
         nc.scalar.copy(out=b_route_rows[:], in_=b_route_t[:])
 
-        def group_w_gate(words, u, g):
+        def transpose_w_gate(words, u, g):
             transpose_words(nc, words, ident[:], [wg_sb[:, 2 * u + e, g * H : (g + 1) * H] for e in range(2)])
-            group_words(nc.scalar.copy, words[:], wg_grouped[(u, g)][:])
+
+        def group_w_gate(copy, words, u, g):
+            group_words(copy, words[:], wg_grouped[(u, g)][:])
 
         first_words = psum.tile([P, 2, HALF], F32, tag="bank", name="wg_words")
-        group_w_gate(first_words, 0, 0)
+        transpose_w_gate(first_words, 0, 0)
+        group_w_gate(nc.scalar.copy, first_words, 0, 0)
+        x_twice = keep.tile([P, SLOTS, P], F32, name="x_twice")
+        nc.scalar.activation(
+            out=x_twice[:], in_=x_grouped[:, tokens_of(0), :].rearrange("q t s -> q s t"), func=ACT.Copy, scale=2.0
+        )
+
+        sum_all = sixteenth[:, 0:1].to_broadcast([P, P])
+        nc.tensor.matmul(out=sums, lhsT=sum_all, rhs=eps[:], start=True, stop=False)
+        nc.tensor.matmul(out=sums, lhsT=sum_all, rhs=twice_r[:], start=False, stop=True)
+        row_inv = keep.tile([P, LIMBS], F32, name="row_inv")
+        nc.vector.reciprocal(out=row_inv[:], in_=sums)
+        to_limb = keep.tile([P, LIMBS], F32, name="to_limb")
+        nc.vector.tensor_tensor(out=to_limb[:], in0=twice_r[:], in1=row_inv[:], op=ALU.mult)
 
         def project(u):
             for n in range(TOKEN_TILES):
@@ -244,22 +259,14 @@ def tile_tpmslimbrouter_pa_s_kernel(
                     stop=True,
                 )
 
-        wg_words = [psum.tile([P, 2, HALF], F32, tag="bank", name="wg_words") for part in wg_parts[1:]]
         proj_ps = [psum.tile([P, BANK], F32, tag="bank", name="proj_ps%d" % n) for n in range(TOKEN_TILES)]
-        group_w_gate(wg_words[0], 0, 1)
+        wg_words = [psum.tile([P, 2, HALF], F32, tag="bank", name="wg_words") for part in wg_parts[1:]]
         project(0)
-
-        sum_all = sixteenth[:, 0:1].to_broadcast([P, P])
-        nc.tensor.matmul(out=sums, lhsT=sum_all, rhs=eps[:], start=True, stop=False)
-        nc.tensor.matmul(out=sums, lhsT=sum_all, rhs=twice_r[:], start=False, stop=True)
-        row_inv = keep.tile([P, LIMBS], F32, name="row_inv")
-        nc.vector.reciprocal(out=row_inv[:], in_=sums)
-        to_limb = keep.tile([P, LIMBS], F32, name="to_limb")
-        nc.vector.tensor_tensor(out=to_limb[:], in0=twice_r[:], in1=row_inv[:], op=ALU.mult)
-
         project(1)
-        group_w_gate(wg_words[1], 1, 0)
-        group_w_gate(wg_words[2], 1, 1)
+        transpose_w_gate(wg_words[0], 0, 1)
+        group_w_gate(nc.scalar.copy, wg_words[0], 0, 1)
+        transpose_w_gate(wg_words[1], 1, 0)
+        group_w_gate(nc.scalar.copy, wg_words[1], 1, 0)
         mixer = keep.tile([P, GROUPS, LIMBS], F32, name="mixer")
         nc.vector.tensor_tensor(
             out=mixer[:],
@@ -275,42 +282,54 @@ def tile_tpmslimbrouter_pa_s_kernel(
                     in1=b_route_rows[:].rearrange("t s q -> t (s q)")[:, half_cols(u)],
                     op=ALU.add,
                 )
-        routed_ps = [psum.tile([P, SLOTS, P], F32, tag="bank", name="routed_ps%d" % n) for n in range(TOKEN_TILES)]
+        routed_ps = {
+            (n, u): psum.tile([P, 2, P], F32, tag="bank", name="routed_ps") for n in range(TOKEN_TILES) for u in range(2)
+        }
 
-        def mix(n):
-            for s in range(SLOTS):
+        def mix(n, u):
+            for e in range(2):
                 nc.tensor.matmul(
-                    out=routed_ps[n][:, s, :],
-                    lhsT=projected[n][:, s, :],
+                    out=routed_ps[(n, u)][:, e, :],
+                    lhsT=projected[n][:, 2 * u + e, :],
                     rhs=mixer[:].rearrange("t a i -> t (a i)"),
                     start=True,
                     stop=True,
                 )
 
-        def round_routed(n):
-            nc.scalar.copy(out=r_grouped[n][:], in_=routed_ps[n][:].rearrange("q s t -> q t s"))
+        def round_routed(n, u):
+            nc.scalar.copy(
+                out=r_grouped[n][:, :, 2 * u : 2 * u + 2], in_=routed_ps[(n, u)][:].rearrange("q e t -> q t e")
+            )
 
         def quantise_routed(n):
             quantise(nc, r_grouped[n][:], r_codes[:, tokens_of(n)], r_scales[:, tokens_of(n)])
 
-        def subtract_x(n):
+        def subtract_x(n, u):
+            slots = slice(2 * u, 2 * u + 2)
             nc.vector.tensor_tensor(
-                out=diff[n][:],
-                in0=routed_ps[n][:],
-                in1=x_grouped[:, tokens_of(n), :].rearrange("q t s -> q s t"),
+                out=diff[n][:, slots, :],
+                in0=routed_ps[(n, u)][:],
+                in1=x_grouped[:, tokens_of(n), slots].rearrange("q t e -> q e t"),
                 op=ALU.subtract,
             )
 
         def quantise_w_gate(u, g):
             quantise(nc, wg_grouped[(u, g)][:], wg_codes[g][:, half_cols(u)], wg_scales[g][:, half_cols(u)])
 
-        for n in range(TOKEN_TILES):
-            mix(n)
-            round_routed(n)
-        for part in wg_parts:
+        for u in range(2):
+            mix(0, u)
+            round_routed(0, u)
+        transpose_w_gate(wg_words[2], 1, 1)
+        group_w_gate(nc.scalar.copy, wg_words[2], 1, 1)
+        for u in range(2):
+            mix(1, u)
+            round_routed(1, u)
+        for part in wg_parts[0:3]:
             quantise_w_gate(*part)
+        subtract_x(0, 0)
         quantise_routed(0)
-        subtract_x(0)
+        subtract_x(0, 1)
+        quantise_w_gate(1, 1)
 
         def gate_pass(out, n, s, g):
             feats = slice(s * P, (s + 1) * P)
@@ -339,6 +358,7 @@ def tile_tpmslimbrouter_pa_s_kernel(
         gates_1 = [psum.tile([P, P], F32, tag="bank", name="gates_1") for s in range(SLOTS)]
         for s in range(SLOTS):
             gate_pass(gates_1[s][:], 1, s, 0)
+        subtract_x(1, 0)
         quantise_routed(1)
         for s in range(SLOTS):
             gate_pass(gates_1[s][:], 1, s, 1)
@@ -360,9 +380,16 @@ def tile_tpmslimbrouter_pa_s_kernel(
                 op1=ALU.mult,
             )
 
-        def transpose_back(moved_t, n, u):
-            for s in (2 * u, 2 * u + 1):
-                nc.tensor.transpose(moved_t[:, s, :], moved[n][:, s, :], ident[:])
+        def transpose_back(moved_t, tile, slots, start, stop):
+            for s in slots:
+                nc.tensor.matmul(
+                    out=moved_t[:, s, :],
+                    lhsT=tile[:, s, :],
+                    rhs=ident[:],
+                    start=start and s == slots[0],
+                    stop=stop and s == slots[-1],
+                    is_transpose=True,
+                )
 
         def add_x_and_store(moved_t, n, h):
             feats = half_cols(h)
@@ -377,15 +404,25 @@ def tile_tpmslimbrouter_pa_s_kernel(
             )
             nc.sync.dma_start(out=out_rows[tokens_of(n), feats], in_=out_sb[:])
 
-        weigh(0, 0)
-        subtract_x(1)
         moved_t = [psum.tile([P, SLOTS, P], F32, tag="bank", name="moved_t%d" % n) for n in range(TOKEN_TILES)]
-        transpose_back(moved_t[0], 0, 0)
+        transpose_back(moved_t[0], x_twice, (0, 1, 2, 3), True, False)
+        weigh(0, 0)
+        subtract_x(1, 1)
+        transpose_back(moved_t[0], moved[0], (0, 1), False, False)
         weigh(0, 1)
-        transpose_back(moved_t[0], 0, 1)
+        transpose_back(moved_t[0], moved[0], (2, 3), False, True)
+        out_0 = keep.tile([P, H], F32, name="out_0")
+        for h in range(2):
+            nc.scalar.activation(
+                out=out_0[:, half_cols(h)].rearrange("t (q s) -> t q s", s=SLOTS),
+                in_=moved_t[0][:, :, h * (P // 2) : (h + 1) * (P // 2)].rearrange("t s q -> t q s"),
+                func=ACT.Copy,
+                scale=0.5,
+            )
+            nc.sync.dma_start(out=out_rows[tokens_of(0), half_cols(h)], in_=out_0[:, half_cols(h)])
         for u in range(2):
             weigh(1, u)
-            transpose_back(moved_t[1], 1, u)
-        for n in range(TOKEN_TILES):
-            for h in range(2):
-                add_x_and_store(moved_t[n], n, h)
+            for s in (2 * u, 2 * u + 1):
+                nc.tensor.transpose(moved_t[1][:, s, :], moved[1][:, s, :], ident[:])
+        for h in range(2):
+            add_x_and_store(moved_t[1], 1, h)

@@ -62,6 +62,8 @@ def tile_tpmslimbrouter_pa_s_kernel(
         warm = keep.tile([P, 1], F32, name="warm")
         nc.vector.memset(warm[:], 0.0)
 
+        b_route_bf = keep.tile([P, SLOTS], BF16, name="b_route_bf")
+        nc.sync.dma_start(out=b_route_bf[:], in_=b_route.rearrange("(q s) -> q s", s=SLOTS))
         x_sb = keep.tile([P, TOKEN_TILES, H], BF16, name="x_sb")
         nc.sync.dma_start(out=x_sb[:], in_=x_rows.rearrange("(n p) k -> p n k", p=P))
         N_POS = LIMBS * COORDS
@@ -70,9 +72,6 @@ def tile_tpmslimbrouter_pa_s_kernel(
         nc.sync.dma_start(out=small_col[16:N_POS, :], in_=pos_flat[16:N_POS, :])
         thr_bf = keep.tile([P, 1], BF16, name="thr_bf")
         nc.scalar.dma_start(out=thr_bf[:], in_=channel_threshold.partition_broadcast(P))
-        b_route_bf = keep.tile([P, SLOTS], BF16, name="b_route_bf")
-        nc.scalar.dma_start(out=b_route_bf[:], in_=b_route.rearrange("(q s) -> q s", s=SLOTS))
-
         wr_sb = keep.tile([P, SLOTS, H], BF16, name="wr_sb")
         wg_sb = keep.tile([P, SLOTS, 2 * H], BF16, name="wg_sb")
         for w_sb, w in ((wr_sb, W_route), (wg_sb, W_gate)):
@@ -81,7 +80,6 @@ def tile_tpmslimbrouter_pa_s_kernel(
                     out=w_sb[:, 2 * u : 2 * u + 2, :],
                     in_=w.rearrange("(q s) k -> q s k", s=SLOTS)[:, 2 * u : 2 * u + 2, :],
                 )
-
         b_gate_bf = keep.tile([P, SLOTS], BF16, name="b_gate_bf")
         nc.sync.dma_start(out=b_gate_bf[:], in_=b_gate.rearrange("(q s) -> q s", s=SLOTS))
 
@@ -103,9 +101,9 @@ def tile_tpmslimbrouter_pa_s_kernel(
         )
         sixteenth = keep.tile([P, 1], F32, name="sixteenth")
         nc.vector.memset(sixteenth[:], 1.0 / GROUPS)
-        eps = keep.tile([P, LIMBS], F32, name="eps")
+        diag_and_eps = keep.tile([P, LIMBS], F32, name="diag_and_eps")
         nc.vector.tensor_scalar(
-            out=eps[:], in0=own_limb[:], scalar1=0.0, scalar2=2.0e-6 * GROUPS / P, op0=ALU.mult, op1=ALU.add
+            out=diag_and_eps[:], in0=own_limb[:], scalar1=2.0 + 2.0e-6, scalar2=None, op0=ALU.mult
         )
 
         PLANES = 2 * COORDS
@@ -167,9 +165,14 @@ def tile_tpmslimbrouter_pa_s_kernel(
         def half_cols(u):
             return slice(u * HALF, (u + 1) * HALF)
 
+        b_route_t = psum.tile([P, SLOTS, P], BF16, tag="bank", name="b_route_t")
+        for s in range(SLOTS):
+            nc.tensor.transpose(b_route_t[:, s, :], b_route_bf[:, s : s + 1].to_broadcast([P, P]), ident_bf[:])
+        b_route_rows = keep.tile([P, SLOTS, P], BF16, name="b_route_rows")
+        nc.scalar.copy(out=b_route_rows[:], in_=b_route_t[:])
         x_words = psum.tile([P, 2, HALF], F32, tag="bank", name="x_words")
-        transpose_words(nc, x_words, ident[:], [x_sb[:, n, :] for n in range(TOKEN_TILES)])
         wr_words = [psum.tile([P, 2, P], F32, tag="bank", name="wr_words") for s in range(SLOTS)]
+        transpose_words(nc, x_words, ident[:], [x_sb[:, n, :] for n in range(TOKEN_TILES)])
         routing_ps = psum.tile([P, BANK], F32, tag="bank", name="routing_ps")
         angles = routing_ps[:, 0:WIDTH]
         sums = routing_ps[:, WIDTH : WIDTH + LIMBS]
@@ -197,9 +200,9 @@ def tile_tpmslimbrouter_pa_s_kernel(
         def quantise_wr(s):
             quantise(nc, wr_grouped[s][:], wr_codes[:, s * P : (s + 1) * P], wr_scales[:, s * P : (s + 1) * P])
 
-        group_words(nc.scalar.copy, wr_words[0][:], wr_grouped[0][:])
         sines = keep.tile([P, WIDTH], F32, name="sines")
         nc.scalar.activation(out=sines[:], in_=minus_frac[:], func=ACT.Sin, scale=-2.0 * math.pi)
+        group_words(nc.scalar.copy, wr_words[0][:], wr_grouped[0][:])
         quantise(nc, x_grouped[:], x_codes[:], x_scales[:])
         gyroid = keep.tile([P, LIMBS], F32, name="gyroid")
         nc.vector.tensor_reduce(
@@ -211,19 +214,24 @@ def tile_tpmslimbrouter_pa_s_kernel(
         quantise_wr(1)
         tanh_f = keep.tile([P, LIMBS], F32, name="tanh_f")
         nc.scalar.activation(out=tanh_f[:], in_=gyroid[:], func=ACT.Tanh, scale=0.5, bias=minus_thr[:, 0:1])
+        twice_r_eps = keep.tile([P, LIMBS], F32, name="twice_r_eps")
+        nc.vector.scalar_tensor_tensor(
+            out=twice_r_eps[:], in0=tanh_f[:], scalar=1.0, in1=diag_and_eps[:], op0=ALU.add, op1=ALU.max
+        )
         twice_r = keep.tile([P, LIMBS], F32, name="twice_r")
         nc.vector.scalar_tensor_tensor(
             out=twice_r[:], in0=tanh_f[:], scalar=1.0, in1=two_on_diag[:], op0=ALU.add, op1=ALU.max
         )
         group_words(nc.scalar.copy, wr_words[3][:], wr_grouped[3][:])
         quantise_wr(2)
+        twice_mixer = keep.tile([P, GROUPS, LIMBS], F32, name="twice_mixer")
+        nc.vector.tensor_tensor(
+            out=twice_mixer[:],
+            in0=own_group[:].unsqueeze(2).to_broadcast([P, GROUPS, LIMBS]),
+            in1=twice_r[:].unsqueeze(1).to_broadcast([P, GROUPS, LIMBS]),
+            op=ALU.mult,
+        )
         quantise_wr(3)
-
-        b_route_t = psum.tile([P, SLOTS, P], BF16, tag="bank", name="b_route_t")
-        for s in range(SLOTS):
-            nc.tensor.transpose(b_route_t[:, s, :], b_route_bf[:, s : s + 1].to_broadcast([P, P]), ident_bf[:])
-        b_route_rows = keep.tile([P, SLOTS, P], BF16, name="b_route_rows")
-        nc.scalar.copy(out=b_route_rows[:], in_=b_route_t[:])
 
         def transpose_w_gate(words, u, g):
             transpose_words(nc, words, ident[:], [wg_sb[:, 2 * u + e, g * H : (g + 1) * H] for e in range(2)])
@@ -239,18 +247,10 @@ def tile_tpmslimbrouter_pa_s_kernel(
             out=x_twice[:], in_=x_grouped[:, tokens_of(0), :].rearrange("q t s -> q s t"), func=ACT.Copy, scale=2.0
         )
 
-        sum_all = sixteenth[:, 0:1].to_broadcast([P, P])
-        nc.tensor.matmul(out=sums, lhsT=sum_all, rhs=eps[:], start=True, stop=False)
-        nc.tensor.matmul(out=sums, lhsT=sum_all, rhs=twice_r[:], start=False, stop=True)
-        row_inv = keep.tile([P, LIMBS], F32, name="row_inv")
-        nc.vector.reciprocal(out=row_inv[:], in_=sums)
-        to_limb = keep.tile([P, LIMBS], F32, name="to_limb")
-        nc.vector.tensor_tensor(out=to_limb[:], in0=twice_r[:], in1=row_inv[:], op=ALU.mult)
-
         def project(u):
             for n in range(TOKEN_TILES):
                 nc.tensor.matmul_mx(
-                    out=proj_ps[n][:, half_cols(u)],
+                    out=proj_ps[(n, u)][:],
                     lhsT=x_codes[:, tokens_of(n)].bitcast(FP8X4),
                     lhsT_scale=x_scales[:, tokens_of(n)],
                     rhs=wr_codes[:, half_cols(u)].bitcast(FP8X4),
@@ -259,29 +259,41 @@ def tile_tpmslimbrouter_pa_s_kernel(
                     stop=True,
                 )
 
-        proj_ps = [psum.tile([P, BANK], F32, tag="bank", name="proj_ps%d" % n) for n in range(TOKEN_TILES)]
+        proj_ps = {
+            (n, u): psum.tile([P, HALF], F32, tag="bank", name="proj_ps") for u in range(2) for n in range(TOKEN_TILES)
+        }
         wg_words = [psum.tile([P, 2, HALF], F32, tag="bank", name="wg_words") for part in wg_parts[1:]]
+        def add_b_route(n, u):
+            nc.vector.tensor_tensor(
+                out=projected[n][:, 2 * u : 2 * u + 2, :].rearrange("t s q -> t (s q)"),
+                in0=proj_ps[(n, u)][:],
+                in1=b_route_rows[:, 2 * u : 2 * u + 2, :].rearrange("t s q -> t (s q)"),
+                op=ALU.add,
+            )
+
         project(0)
-        project(1)
+        nc.tensor.matmul(
+            out=sums, lhsT=sixteenth[:, 0:1].to_broadcast([P, P]), rhs=twice_r_eps[:], start=True, stop=True
+        )
         transpose_w_gate(wg_words[0], 0, 1)
         group_w_gate(nc.scalar.copy, wg_words[0], 0, 1)
-        transpose_w_gate(wg_words[1], 1, 0)
-        group_w_gate(nc.scalar.copy, wg_words[1], 1, 0)
+        project(1)
+        add_b_route(0, 0)
+        row_inv = keep.tile([P, LIMBS], F32, name="row_inv")
+        nc.vector.reciprocal(out=row_inv[:], in_=sums)
         mixer = keep.tile([P, GROUPS, LIMBS], F32, name="mixer")
         nc.vector.tensor_tensor(
             out=mixer[:],
-            in0=own_group[:].unsqueeze(2).to_broadcast([P, GROUPS, LIMBS]),
-            in1=to_limb[:].unsqueeze(1).to_broadcast([P, GROUPS, LIMBS]),
+            in0=twice_mixer[:],
+            in1=row_inv[:].unsqueeze(1).to_broadcast([P, GROUPS, LIMBS]),
             op=ALU.mult,
         )
-        for n in range(TOKEN_TILES):
-            for u in range(2):
-                nc.vector.tensor_tensor(
-                    out=projected[n][:].rearrange("t s q -> t (s q)")[:, half_cols(u)],
-                    in0=proj_ps[n][:, half_cols(u)],
-                    in1=b_route_rows[:].rearrange("t s q -> t (s q)")[:, half_cols(u)],
-                    op=ALU.add,
-                )
+        add_b_route(0, 1)
+        for u in range(2):
+            add_b_route(1, u)
+        transpose_w_gate(wg_words[1], 1, 0)
+        group_w_gate(nc.scalar.copy, wg_words[1], 1, 0)
+
         routed_ps = {
             (n, u): psum.tile([P, 2, P], F32, tag="bank", name="routed_ps") for n in range(TOKEN_TILES) for u in range(2)
         }
@@ -369,8 +381,7 @@ def tile_tpmslimbrouter_pa_s_kernel(
 
         moved = [keep.tile([P, SLOTS, P], F32, name="moved%d" % n) for n in range(TOKEN_TILES)]
 
-        def weigh(n, u):
-            slots = slice(2 * u, 2 * u + 2)
+        def weigh(n, slots):
             nc.vector.scalar_tensor_tensor(
                 out=moved[n][:, slots, :].rearrange("q e t -> q (e t)"),
                 in0=tanh_g[n][:, slots, :].rearrange("q e t -> q (e t)"),
@@ -406,10 +417,10 @@ def tile_tpmslimbrouter_pa_s_kernel(
 
         moved_t = [psum.tile([P, SLOTS, P], F32, tag="bank", name="moved_t%d" % n) for n in range(TOKEN_TILES)]
         transpose_back(moved_t[0], x_twice, (0, 1, 2, 3), True, False)
-        weigh(0, 0)
+        weigh(0, slice(0, 2))
         subtract_x(1, 1)
         transpose_back(moved_t[0], moved[0], (0, 1), False, False)
-        weigh(0, 1)
+        weigh(0, slice(2, 4))
         transpose_back(moved_t[0], moved[0], (2, 3), False, True)
         out_0 = keep.tile([P, H], F32, name="out_0")
         for h in range(2):
@@ -420,9 +431,8 @@ def tile_tpmslimbrouter_pa_s_kernel(
                 scale=0.5,
             )
             nc.sync.dma_start(out=out_rows[tokens_of(0), half_cols(h)], in_=out_0[:, half_cols(h)])
-        for u in range(2):
-            weigh(1, u)
-            for s in (2 * u, 2 * u + 1):
-                nc.tensor.transpose(moved_t[1][:, s, :], moved[1][:, s, :], ident[:])
+        for s in range(SLOTS):
+            weigh(1, slice(s, s + 1))
+            nc.tensor.transpose(moved_t[1][:, s, :], moved[1][:, s, :], ident[:])
         for h in range(2):
             add_x_and_store(moved_t[1], 1, h)

@@ -64,12 +64,12 @@ def tile_tpmslimbrouter_pa_s_kernel(
 
         b_route_bf = keep.tile([P, SLOTS], BF16, name="b_route_bf")
         nc.sync.dma_start(out=b_route_bf[:], in_=b_route.rearrange("(q s) -> q s", s=SLOTS))
-        x_sb = keep.tile([P, TOKEN_TILES, H], BF16, name="x_sb")
-        nc.sync.dma_start(out=x_sb[:], in_=x_rows.rearrange("(n p) k -> p n k", p=P))
         N_POS = LIMBS * COORDS
         pos_flat = limb_positions.rearrange("i c -> (i c)").unsqueeze(1)
         nc.sync.dma_start(out=small_col[0:16, :], in_=pos_flat[0:16, :])
         nc.sync.dma_start(out=small_col[16:N_POS, :], in_=pos_flat[16:N_POS, :])
+        x_sb = keep.tile([P, TOKEN_TILES, H], BF16, name="x_sb")
+        nc.sync.dma_start(out=x_sb[:], in_=x_rows.rearrange("(n p) k -> p n k", p=P))
         thr_bf = keep.tile([P, 1], BF16, name="thr_bf")
         nc.scalar.dma_start(out=thr_bf[:], in_=channel_threshold.partition_broadcast(P))
         wr_sb = keep.tile([P, SLOTS, H], BF16, name="wr_sb")
@@ -85,27 +85,10 @@ def tile_tpmslimbrouter_pa_s_kernel(
 
         nc.scalar.activation(out=warm[:], in_=warm[:], func=ACT.Silu)
 
-        own_limb = keep.tile([P, LIMBS], F32, name="own_limb")
-        nc.vector.tensor_reduce(
-            out=own_limb[:], in_=ident[:].rearrange("p (a j) -> p j a", j=LIMBS), axis=AXIS_X, op=ALU.add
-        )
-        own_group = keep.tile([P, GROUPS], F32, name="own_group")
-        nc.vector.tensor_reduce(
-            out=own_group[:], in_=ident[:].rearrange("p (a j) -> p a j", j=LIMBS), axis=AXIS_X, op=ALU.add
-        )
-        two_on_diag = keep.tile([P, LIMBS], F32, name="two_on_diag")
-        nc.vector.tensor_scalar(out=two_on_diag[:], in0=own_limb[:], scalar1=2.0, scalar2=None, op0=ALU.mult)
         coord_of = keep.tile([P, LIMBS], F32, name="coord_of")
         nc.vector.tensor_reduce(
             out=coord_of[:], in_=ident[:, 0:N_POS].rearrange("k (i c) -> k i c", c=COORDS), axis=AXIS_X, op=ALU.add
         )
-        sixteenth = keep.tile([P, 1], F32, name="sixteenth")
-        nc.vector.memset(sixteenth[:], 1.0 / GROUPS)
-        diag_and_eps = keep.tile([P, LIMBS], F32, name="diag_and_eps")
-        nc.vector.tensor_scalar(
-            out=diag_and_eps[:], in0=own_limb[:], scalar1=2.0 + 2.0e-6, scalar2=None, op0=ALU.mult
-        )
-
         PLANES = 2 * COORDS
         WIDTH = PLANES * LIMBS
         unit = ident[:, 0:N_POS].rearrange("k (i c) -> k c i", c=COORDS)
@@ -133,6 +116,23 @@ def tile_tpmslimbrouter_pa_s_kernel(
         )
         minus_thr = keep.tile([P, 1], F32, name="minus_thr")
         nc.vector.tensor_scalar(out=minus_thr[:], in0=thr_bf[:], scalar1=-1.0, scalar2=None, op0=ALU.mult)
+
+        own_limb = keep.tile([P, LIMBS], F32, name="own_limb")
+        nc.vector.tensor_reduce(
+            out=own_limb[:], in_=ident[:].rearrange("p (a j) -> p j a", j=LIMBS), axis=AXIS_X, op=ALU.add
+        )
+        own_group = keep.tile([P, GROUPS], F32, name="own_group")
+        nc.vector.tensor_reduce(
+            out=own_group[:], in_=ident[:].rearrange("p (a j) -> p a j", j=LIMBS), axis=AXIS_X, op=ALU.add
+        )
+        two_on_diag = keep.tile([P, LIMBS], F32, name="two_on_diag")
+        nc.vector.tensor_scalar(out=two_on_diag[:], in0=own_limb[:], scalar1=2.0, scalar2=None, op0=ALU.mult)
+        sixteenth = keep.tile([P, 1], F32, name="sixteenth")
+        nc.vector.memset(sixteenth[:], 1.0 / GROUPS)
+        diag_and_eps = keep.tile([P, LIMBS], F32, name="diag_and_eps")
+        nc.vector.tensor_scalar(
+            out=diag_and_eps[:], in0=own_limb[:], scalar1=2.0 + 2.0e-6, scalar2=None, op0=ALU.mult
+        )
 
         ident_bf = keep.tile([P, P], BF16, name="ident_bf")
         nc.gpsimd.tensor_copy(out=ident_bf[:], in_=ident[:])
@@ -172,7 +172,6 @@ def tile_tpmslimbrouter_pa_s_kernel(
         nc.scalar.copy(out=b_route_rows[:], in_=b_route_t[:])
         x_words = psum.tile([P, 2, HALF], F32, tag="bank", name="x_words")
         wr_words = [psum.tile([P, 2, P], F32, tag="bank", name="wr_words") for s in range(SLOTS)]
-        transpose_words(nc, x_words, ident[:], [x_sb[:, n, :] for n in range(TOKEN_TILES)])
         routing_ps = psum.tile([P, BANK], F32, tag="bank", name="routing_ps")
         angles = routing_ps[:, 0:WIDTH]
         sums = routing_ps[:, WIDTH : WIDTH + LIMBS]
@@ -182,7 +181,7 @@ def tile_tpmslimbrouter_pa_s_kernel(
         nc.tensor.matmul(
             out=angles, lhsT=small_own[:].rearrange("k a j -> k (a j)"), rhs=of_own[:], start=False, stop=True
         )
-        group_words(nc.scalar.copy, x_words[:], x_grouped[:])
+        transpose_words(nc, x_words, ident[:], [x_sb[:, n, :] for n in range(TOKEN_TILES)])
         TURN = 1.0 / (4.0 * math.pi)
         turns = keep.tile([P, WIDTH], F32, name="turns")
         nc.vector.tensor_scalar(out=turns[:], in0=angles, scalar1=TURN, scalar2=None, op0=ALU.mult)
@@ -202,18 +201,20 @@ def tile_tpmslimbrouter_pa_s_kernel(
 
         sines = keep.tile([P, WIDTH], F32, name="sines")
         nc.scalar.activation(out=sines[:], in_=minus_frac[:], func=ACT.Sin, scale=-2.0 * math.pi)
+        group_words(nc.vector.tensor_copy, x_words[:], x_grouped[:])
         group_words(nc.scalar.copy, wr_words[0][:], wr_grouped[0][:])
-        quantise(nc, x_grouped[:], x_codes[:], x_scales[:])
         gyroid = keep.tile([P, LIMBS], F32, name="gyroid")
         nc.vector.tensor_reduce(
             out=gyroid[:], in_=sines[:].rearrange("p (w i) -> p i w", i=LIMBS), axis=AXIS_X, op=ALU.add
         )
-        group_words(nc.vector.tensor_copy, wr_words[1][:], wr_grouped[1][:])
-        group_words(nc.scalar.copy, wr_words[2][:], wr_grouped[2][:])
-        quantise_wr(0)
-        quantise_wr(1)
+        quantise(nc, x_grouped[:], x_codes[:], x_scales[:])
+        group_words(nc.scalar.copy, wr_words[1][:], wr_grouped[1][:])
         tanh_f = keep.tile([P, LIMBS], F32, name="tanh_f")
         nc.scalar.activation(out=tanh_f[:], in_=gyroid[:], func=ACT.Tanh, scale=0.5, bias=minus_thr[:, 0:1])
+        for s in range(2, SLOTS):
+            group_words(nc.scalar.copy, wr_words[s][:], wr_grouped[s][:])
+        for s in range(2):
+            quantise_wr(s)
         twice_r_eps = keep.tile([P, LIMBS], F32, name="twice_r_eps")
         nc.vector.scalar_tensor_tensor(
             out=twice_r_eps[:], in0=tanh_f[:], scalar=1.0, in1=diag_and_eps[:], op0=ALU.add, op1=ALU.max
@@ -222,7 +223,6 @@ def tile_tpmslimbrouter_pa_s_kernel(
         nc.vector.scalar_tensor_tensor(
             out=twice_r[:], in0=tanh_f[:], scalar=1.0, in1=two_on_diag[:], op0=ALU.add, op1=ALU.max
         )
-        group_words(nc.scalar.copy, wr_words[3][:], wr_grouped[3][:])
         quantise_wr(2)
         twice_mixer = keep.tile([P, GROUPS, LIMBS], F32, name="twice_mixer")
         nc.vector.tensor_tensor(
@@ -275,8 +275,6 @@ def tile_tpmslimbrouter_pa_s_kernel(
         nc.tensor.matmul(
             out=sums, lhsT=sixteenth[:, 0:1].to_broadcast([P, P]), rhs=twice_r_eps[:], start=True, stop=True
         )
-        transpose_w_gate(wg_words[0], 0, 1)
-        group_w_gate(nc.scalar.copy, wg_words[0], 0, 1)
         project(1)
         add_b_route(0, 0)
         row_inv = keep.tile([P, LIMBS], F32, name="row_inv")
@@ -289,8 +287,10 @@ def tile_tpmslimbrouter_pa_s_kernel(
             op=ALU.mult,
         )
         add_b_route(0, 1)
-        for u in range(2):
-            add_b_route(1, u)
+        add_b_route(1, 0)
+        add_b_route(1, 1)
+        transpose_w_gate(wg_words[0], 0, 1)
+        group_w_gate(nc.scalar.copy, wg_words[0], 0, 1)
         transpose_w_gate(wg_words[1], 1, 0)
         group_w_gate(nc.scalar.copy, wg_words[1], 1, 0)
 

@@ -74,12 +74,18 @@ def tile_tpmslimbrouter_pa_s_kernel(
         nc.scalar.dma_start(out=thr_bf[:], in_=channel_threshold.partition_broadcast(P))
         wr_sb = keep.tile([P, SLOTS, H], BF16, name="wr_sb")
         wg_sb = keep.tile([P, SLOTS, 2 * H], BF16, name="wg_sb")
-        for w_sb, w in ((wr_sb, W_route), (wg_sb, W_gate)):
-            for u in range(2):
-                nc.sync.dma_start(
-                    out=w_sb[:, 2 * u : 2 * u + 2, :],
-                    in_=w.rearrange("(q s) k -> q s k", s=SLOTS)[:, 2 * u : 2 * u + 2, :],
-                )
+
+        def load_rows(w_sb, w, u, cols):
+            nc.sync.dma_start(
+                out=w_sb[:, 2 * u : 2 * u + 2, cols],
+                in_=w.rearrange("(q s) k -> q s k", s=SLOTS)[:, 2 * u : 2 * u + 2, cols],
+            )
+
+        for u in range(2):
+            load_rows(wr_sb, W_route, u, slice(0, H))
+        for g in range(2):
+            load_rows(wg_sb, W_gate, 0, slice(g * H, (g + 1) * H))
+        load_rows(wg_sb, W_gate, 1, slice(0, 2 * H))
         b_gate_bf = keep.tile([P, SLOTS], BF16, name="b_gate_bf")
         nc.sync.dma_start(out=b_gate_bf[:], in_=b_gate.rearrange("(q s) -> q s", s=SLOTS))
 
@@ -239,9 +245,10 @@ def tile_tpmslimbrouter_pa_s_kernel(
         def group_w_gate(copy, words, u, g):
             group_words(copy, words[:], wg_grouped[(u, g)][:])
 
-        first_words = psum.tile([P, 2, HALF], F32, tag="bank", name="wg_words")
-        transpose_w_gate(first_words, 0, 0)
-        group_w_gate(nc.scalar.copy, first_words, 0, 0)
+        first_words = [psum.tile([P, 2, HALF], F32, tag="bank", name="wg_words") for part in wg_parts[:2]]
+        for words, part in zip(first_words, wg_parts):
+            transpose_w_gate(words, *part)
+            group_w_gate(nc.scalar.copy, words, *part)
         x_twice = keep.tile([P, SLOTS, P], F32, name="x_twice")
         nc.scalar.activation(
             out=x_twice[:], in_=x_grouped[:, tokens_of(0), :].rearrange("q t s -> q s t"), func=ACT.Copy, scale=2.0
@@ -262,7 +269,7 @@ def tile_tpmslimbrouter_pa_s_kernel(
         proj_ps = {
             (n, u): psum.tile([P, HALF], F32, tag="bank", name="proj_ps") for u in range(2) for n in range(TOKEN_TILES)
         }
-        wg_words = [psum.tile([P, 2, HALF], F32, tag="bank", name="wg_words") for part in wg_parts[1:]]
+        late_words = [psum.tile([P, 2, HALF], F32, tag="bank", name="wg_words") for part in wg_parts[2:]]
         def add_b_route(n, u):
             nc.vector.tensor_tensor(
                 out=projected[n][:, 2 * u : 2 * u + 2, :].rearrange("t s q -> t (s q)"),
@@ -271,14 +278,14 @@ def tile_tpmslimbrouter_pa_s_kernel(
                 op=ALU.add,
             )
 
-        project(0)
         nc.tensor.matmul(
             out=sums, lhsT=sixteenth[:, 0:1].to_broadcast([P, P]), rhs=twice_r_eps[:], start=True, stop=True
         )
+        project(0)
         project(1)
-        add_b_route(0, 0)
         row_inv = keep.tile([P, LIMBS], F32, name="row_inv")
         nc.vector.reciprocal(out=row_inv[:], in_=sums)
+        add_b_route(0, 0)
         mixer = keep.tile([P, GROUPS, LIMBS], F32, name="mixer")
         nc.vector.tensor_tensor(
             out=mixer[:],
@@ -289,10 +296,8 @@ def tile_tpmslimbrouter_pa_s_kernel(
         add_b_route(0, 1)
         add_b_route(1, 0)
         add_b_route(1, 1)
-        transpose_w_gate(wg_words[0], 0, 1)
-        group_w_gate(nc.scalar.copy, wg_words[0], 0, 1)
-        transpose_w_gate(wg_words[1], 1, 0)
-        group_w_gate(nc.scalar.copy, wg_words[1], 1, 0)
+        transpose_w_gate(late_words[0], 1, 0)
+        group_w_gate(nc.scalar.copy, late_words[0], 1, 0)
 
         routed_ps = {
             (n, u): psum.tile([P, 2, P], F32, tag="bank", name="routed_ps") for n in range(TOKEN_TILES) for u in range(2)
@@ -331,8 +336,8 @@ def tile_tpmslimbrouter_pa_s_kernel(
         for u in range(2):
             mix(0, u)
             round_routed(0, u)
-        transpose_w_gate(wg_words[2], 1, 1)
-        group_w_gate(nc.scalar.copy, wg_words[2], 1, 1)
+        transpose_w_gate(late_words[1], 1, 1)
+        group_w_gate(nc.scalar.copy, late_words[1], 1, 1)
         for u in range(2):
             mix(1, u)
             round_routed(1, u)

@@ -230,6 +230,7 @@ def tile_tpmslimbrouter_pa_s_kernel(
             out=twice_r[:], in0=tanh_f[:], scalar=1.0, in1=two_on_diag[:], op0=ALU.add, op1=ALU.max
         )
         quantise_wr(2)
+        quantise_wr(3)
         twice_mixer = keep.tile([P, GROUPS, LIMBS], F32, name="twice_mixer")
         nc.vector.tensor_tensor(
             out=twice_mixer[:],
@@ -237,7 +238,6 @@ def tile_tpmslimbrouter_pa_s_kernel(
             in1=twice_r[:].unsqueeze(1).to_broadcast([P, GROUPS, LIMBS]),
             op=ALU.mult,
         )
-        quantise_wr(3)
 
         def transpose_w_gate(words, u, g):
             transpose_words(nc, words, ident[:], [wg_sb[:, 2 * u + e, g * H : (g + 1) * H] for e in range(2)])
@@ -296,8 +296,9 @@ def tile_tpmslimbrouter_pa_s_kernel(
         add_b_route(0, 1)
         add_b_route(1, 0)
         add_b_route(1, 1)
-        transpose_w_gate(late_words[0], 1, 0)
-        group_w_gate(nc.scalar.copy, late_words[0], 1, 0)
+        for words, part in zip(late_words, wg_parts[2:]):
+            transpose_w_gate(words, *part)
+            group_w_gate(nc.scalar.copy, words, *part)
 
         routed_ps = {
             (n, u): psum.tile([P, 2, P], F32, tag="bank", name="routed_ps") for n in range(TOKEN_TILES) for u in range(2)
@@ -336,17 +337,14 @@ def tile_tpmslimbrouter_pa_s_kernel(
         for u in range(2):
             mix(0, u)
             round_routed(0, u)
-        transpose_w_gate(late_words[1], 1, 1)
-        group_w_gate(nc.scalar.copy, late_words[1], 1, 1)
         for u in range(2):
             mix(1, u)
             round_routed(1, u)
-        for part in wg_parts[0:3]:
+        for part in wg_parts:
             quantise_w_gate(*part)
         subtract_x(0, 0)
         quantise_routed(0)
         subtract_x(0, 1)
-        quantise_w_gate(1, 1)
 
         def gate_pass(out, n, s, g):
             feats = slice(s * P, (s + 1) * P)
@@ -377,6 +375,7 @@ def tile_tpmslimbrouter_pa_s_kernel(
             gate_pass(gates_1[s][:], 1, s, 0)
         subtract_x(1, 0)
         quantise_routed(1)
+        subtract_x(1, 1)
         for s in range(SLOTS):
             gate_pass(gates_1[s][:], 1, s, 1)
         for s in range(SLOTS):
@@ -423,7 +422,6 @@ def tile_tpmslimbrouter_pa_s_kernel(
         moved_t = [psum.tile([P, SLOTS, P], F32, tag="bank", name="moved_t%d" % n) for n in range(TOKEN_TILES)]
         transpose_back(moved_t[0], x_twice, (0, 1, 2, 3), True, False)
         weigh(0, slice(0, 2))
-        subtract_x(1, 1)
         transpose_back(moved_t[0], moved[0], (0, 1), False, False)
         weigh(0, slice(2, 4))
         transpose_back(moved_t[0], moved[0], (2, 3), False, True)

@@ -70,8 +70,7 @@ def tile_tpmslimbrouter_pa_s_kernel(
         nc.sync.dma_start(out=small_col[16:N_POS, :], in_=pos_flat[16:N_POS, :])
         x_sb = keep.tile([P, TOKEN_TILES, H], BF16, name="x_sb")
         nc.sync.dma_start(out=x_sb[:], in_=x_rows.rearrange("(n p) k -> p n k", p=P))
-        thr_bf = keep.tile([P, 1], BF16, name="thr_bf")
-        nc.scalar.dma_start(out=thr_bf[:], in_=channel_threshold.partition_broadcast(P))
+        nc.scalar.dma_start(out=small_col[N_POS : N_POS + 1, :], in_=channel_threshold.unsqueeze(1))
         wr_sb = keep.tile([P, SLOTS, H], BF16, name="wr_sb")
         wg_sb = keep.tile([P, SLOTS, 2 * H], BF16, name="wg_sb")
 
@@ -98,18 +97,26 @@ def tile_tpmslimbrouter_pa_s_kernel(
         PLANES = 2 * COORDS
         WIDTH = PLANES * LIMBS
         unit = ident[:, 0:N_POS].rearrange("k (i c) -> k c i", c=COORDS)
-        of_limb = keep.tile([P, WIDTH], BF16, name="of_limb")
-        planes = of_limb[:].rearrange("k (g c i) -> k g c i", g=2, c=COORDS)
+        of_limb = keep.tile([P, WIDTH + 1], BF16, name="of_limb")
+        planes = of_limb[:, 0:WIDTH].rearrange("k (g c i) -> k g c i", g=2, c=COORDS)
         for g, op in enumerate((ALU.add, ALU.subtract)):
             nc.vector.tensor_tensor(out=planes[:, g, 0:2, :], in0=unit[:, 0:2, :], in1=unit[:, 1:3, :], op=op)
             nc.vector.tensor_tensor(out=planes[:, g, 2, :], in0=unit[:, 2, :], in1=unit[:, 0, :], op=op)
         own_planes = keep.tile([P, PLANES], F32, name="own_planes")
         nc.vector.tensor_reduce(
-            out=own_planes[:], in_=of_limb[:].rearrange("k (w i) -> k w i", i=LIMBS), axis=AXIS_X, op=ALU.add
+            out=own_planes[:], in_=of_limb[:, 0:WIDTH].rearrange("k (w i) -> k w i", i=LIMBS), axis=AXIS_X, op=ALU.add
         )
-        of_own = keep.tile([P, WIDTH], BF16, name="of_own")
+        nc.vector.tensor_scalar(
+            out=of_limb[:, WIDTH : WIDTH + 1],
+            in0=ident[:, N_POS : N_POS + 1],
+            scalar1=-1.0,
+            scalar2=None,
+            op0=ALU.mult,
+        )
+        of_own = keep.tile([P, WIDTH + 1], BF16, name="of_own")
+        nc.vector.memset(of_own[:, WIDTH : WIDTH + 1], 0.0)
         nc.vector.tensor_copy(
-            out=of_own[:].rearrange("k (w i) -> k w i", i=LIMBS),
+            out=of_own[:, 0:WIDTH].rearrange("k (w i) -> k w i", i=LIMBS),
             in_=own_planes[:].unsqueeze(2).to_broadcast([P, PLANES, LIMBS]),
         )
         small_own = keep.tile([P, GROUPS, LIMBS], BF16, name="small_own")
@@ -120,8 +127,6 @@ def tile_tpmslimbrouter_pa_s_kernel(
             scalar2=None,
             op0=ALU.mult,
         )
-        minus_thr = keep.tile([P, 1], F32, name="minus_thr")
-        nc.vector.tensor_scalar(out=minus_thr[:], in0=thr_bf[:], scalar1=-1.0, scalar2=None, op0=ALU.mult)
 
         own_limb = keep.tile([P, LIMBS], F32, name="own_limb")
         nc.vector.tensor_reduce(
@@ -179,13 +184,14 @@ def tile_tpmslimbrouter_pa_s_kernel(
         x_words = psum.tile([P, 2, HALF], F32, tag="bank", name="x_words")
         wr_words = [psum.tile([P, 2, P], F32, tag="bank", name="wr_words") for s in range(SLOTS)]
         routing_ps = psum.tile([P, BANK], F32, tag="bank", name="routing_ps")
+        angles_thr = routing_ps[:, 0 : WIDTH + 1]
         angles = routing_ps[:, 0:WIDTH]
-        sums = routing_ps[:, WIDTH : WIDTH + LIMBS]
+        sums = routing_ps[:, 2 * WIDTH : 2 * WIDTH + LIMBS]
         nc.tensor.matmul(
-            out=angles, lhsT=small_col[:, 0:1].to_broadcast([P, P]), rhs=of_limb[:], start=True, stop=False
+            out=angles_thr, lhsT=small_col[:, 0:1].to_broadcast([P, P]), rhs=of_limb[:], start=True, stop=False
         )
         nc.tensor.matmul(
-            out=angles, lhsT=small_own[:].rearrange("k a j -> k (a j)"), rhs=of_own[:], start=False, stop=True
+            out=angles_thr, lhsT=small_own[:].rearrange("k a j -> k (a j)"), rhs=of_own[:], start=False, stop=True
         )
         transpose_words(nc, x_words, ident[:], [x_sb[:, n, :] for n in range(TOKEN_TILES)])
         TURN = 1.0 / (4.0 * math.pi)
@@ -199,6 +205,8 @@ def tile_tpmslimbrouter_pa_s_kernel(
         nc.vector.scalar_tensor_tensor(
             out=minus_frac[:], in0=rounded[:], scalar=ROUND_MAGIC, in1=turns[:], op0=ALU.subtract, op1=ALU.subtract
         )
+        minus_thr = keep.tile([P, 1], F32, name="minus_thr")
+        nc.vector.tensor_copy(out=minus_thr[:], in_=routing_ps[:, WIDTH : WIDTH + 1])
         for s in range(SLOTS):
             transpose_words(nc, wr_words[s], ident[:], [wr_sb[:, s, :]])
 

import math
from contextlib import ExitStack

import concourse.mybir as mybir
from concourse.masks import make_identity

F32 = mybir.dt.float32
BF16 = mybir.dt.bfloat16
U32 = mybir.dt.uint32
U8 = mybir.dt.uint8
FP8X4 = mybir.dt.float8_e4m3fn_x4
ALU = mybir.AluOpType
ACT = mybir.ActivationFunctionType
AXIS_X = mybir.AxisListType.X

P = 128
TOKENS = 256
TOKEN_TILES = TOKENS // P
LIMBS = 8
GROUPS = P // LIMBS
COORDS = 3
H = 512
SLOTS = 4
BANK = 512
HALF = BANK // 2
ROUND_MAGIC = 1.5 * 2.0**23

FLOPS = 2 * TOKENS * H * H + 2 * TOKENS * 2 * H * H + 2 * TOKENS * LIMBS * H


def transpose_words(nc, bank, ident, row_blocks):
    for b, rows in enumerate(row_blocks):
        words = rows.bitcast(F32)
        for u in range(2):
            nc.tensor.transpose(bank[:, u, b * P : (b + 1) * P], words[:, u : 2 * P : 2], ident)


def group_words(copy, bank, grouped):
    copy(out=grouped.bitcast(F32), in_=bank.rearrange("q u c -> q c u"))


def quantise(nc, grouped, codes, scales):
    nc.vector.quantize_mx(out=codes.bitcast(FP8X4), scales=scales, in_=grouped.rearrange("q c s -> q (c s)"))


def tile_tpmslimbrouter_pa_s_kernel(
    tc, x, limb_positions, channel_threshold, W_route, b_route, W_gate, b_gate, out
):
    nc = tc.nc
    x_rows = x.flatten_outer_dims()
    out_rows = out.flatten_outer_dims()

    with ExitStack() as ctx:
        keep = ctx.enter_context(tc.tile_pool(name="keep", bufs=1))
        psum = ctx.enter_context(tc.psum_pool(name="psum", bufs=8))
        ctx.enter_context(tc.manual_schedule())

        small_col = keep.tile([P, 1], BF16, name="small_col")
        nc.gpsimd.memset(small_col[:], 0.0)
        ident = keep.tile([P, P], F32, name="ident")
        make_identity(nc, ident[:])
        warm = keep.tile([P, 1], F32, name="warm")
        nc.vector.memset(warm[:], 0.0)

        b_route_bf = keep.tile([P, SLOTS], BF16, name="b_route_bf")
        nc.sync.dma_start(out=b_route_bf[:], in_=b_route.rearrange("(q s) -> q s", s=SLOTS))
        N_POS = LIMBS * COORDS
        pos_flat = limb_positions.rearrange("i c -> (i c)").unsqueeze(1)
        nc.sync.dma_start(out=small_col[0:16, :], in_=pos_flat[0:16, :])
        nc.sync.dma_start(out=small_col[16:N_POS, :], in_=pos_flat[16:N_POS, :])
        x_sb = keep.tile([P, TOKEN_TILES, H], BF16, name="x_sb")
        nc.sync.dma_start(out=x_sb[:], in_=x_rows.rearrange("(n p) k -> p n k", p=P))
        nc.scalar.dma_start(out=small_col[N_POS : N_POS + 1, :], in_=channel_threshold.unsqueeze(1))
        wr_sb = keep.tile([P, SLOTS, H], BF16, name="wr_sb")
        wg_sb = keep.tile([P, SLOTS, 2 * H], BF16, name="wg_sb")

        def load_rows(w_sb, w, u, cols):
            nc.sync.dma_start(
                out=w_sb[:, 2 * u : 2 * u + 2, cols],
                in_=w.rearrange("(q s) k -> q s k", s=SLOTS)[:, 2 * u : 2 * u + 2, cols],
            )

        for u in range(2):
            load_rows(wr_sb, W_route, u, slice(0, H))
        for g in range(2):
            load_rows(wg_sb, W_gate, 0, slice(g * H, (g + 1) * H))
        load_rows(wg_sb, W_gate, 1, slice(0, 2 * H))
        b_gate_bf = keep.tile([P, SLOTS], BF16, name="b_gate_bf")
        nc.sync.dma_start(out=b_gate_bf[:], in_=b_gate.rearrange("(q s) -> q s", s=SLOTS))

        nc.scalar.activation(out=warm[:], in_=warm[:], func=ACT.Silu)

        coord_of = keep.tile([P, LIMBS], F32, name="coord_of")
        nc.vector.tensor_reduce(
            out=coord_of[:], in_=ident[:, 0:N_POS].rearrange("k (i c) -> k i c", c=COORDS), axis=AXIS_X, op=ALU.add
        )
        PLANES = 2 * COORDS
        WIDTH = PLANES * LIMBS
        unit = ident[:, 0:N_POS].rearrange("k (i c) -> k c i", c=COORDS)
        of_limb = keep.tile([P, WIDTH + 1], BF16, name="of_limb")
        planes = of_limb[:, 0:WIDTH].rearrange("k (g c i) -> k g c i", g=2, c=COORDS)
        for g, op in enumerate((ALU.add, ALU.subtract)):
            nc.vector.tensor_tensor(out=planes[:, g, 0:2, :], in0=unit[:, 0:2, :], in1=unit[:, 1:3, :], op=op)
            nc.vector.tensor_tensor(out=planes[:, g, 2, :], in0=unit[:, 2, :], in1=unit[:, 0, :], op=op)
        own_planes = keep.tile([P, PLANES], F32, name="own_planes")
        nc.vector.tensor_reduce(
            out=own_planes[:], in_=of_limb[:, 0:WIDTH].rearrange("k (w i) -> k w i", i=LIMBS), axis=AXIS_X, op=ALU.add
        )
        nc.vector.tensor_scalar(
            out=of_limb[:, WIDTH : WIDTH + 1],
            in0=ident[:, N_POS : N_POS + 1],
            scalar1=-1.0,
            scalar2=None,
            op0=ALU.mult,
        )
        of_own = keep.tile([P, WIDTH + 1], BF16, name="of_own")
        nc.vector.memset(of_own[:, WIDTH : WIDTH + 1], 0.0)
        nc.vector.tensor_copy(
            out=of_own[:, 0:WIDTH].rearrange("k (w i) -> k w i", i=LIMBS),
            in_=own_planes[:].unsqueeze(2).to_broadcast([P, PLANES, LIMBS]),
        )
        small_own = keep.tile([P, GROUPS, LIMBS], BF16, name="small_own")
        nc.vector.tensor_scalar(
            out=small_own[:],
            in0=coord_of[:].unsqueeze(1).to_broadcast([P, GROUPS, LIMBS]),
            scalar1=small_col[:, 0:1],
            scalar2=None,
            op0=ALU.mult,
        )

        own_limb = keep.tile([P, LIMBS], F32, name="own_limb")
        nc.vector.tensor_reduce(
            out=own_limb[:], in_=ident[:].rearrange("p (a j) -> p j a", j=LIMBS), axis=AXIS_X, op=ALU.add
        )
        own_group = keep.tile([P, GROUPS], F32, name="own_group")
        nc.vector.tensor_reduce(
            out=own_group[:], in_=ident[:].rearrange("p (a j) -> p a j", j=LIMBS), axis=AXIS_X, op=ALU.add
        )
        two_on_diag = keep.tile([P, LIMBS], F32, name="two_on_diag")
        nc.vector.tensor_scalar(out=two_on_diag[:], in0=own_limb[:], scalar1=2.0, scalar2=None, op0=ALU.mult)
        sixteenth = keep.tile([P, 1], F32, name="sixteenth")
        nc.vector.memset(sixteenth[:], 1.0 / GROUPS)
        diag_and_eps = keep.tile([P, LIMBS], F32, name="diag_and_eps")
        nc.vector.tensor_scalar(
            out=diag_and_eps[:], in0=own_limb[:], scalar1=2.0 + 2.0e-6, scalar2=None, op0=ALU.mult
        )

        ident_bf = keep.tile([P, P], BF16, name="ident_bf")
        nc.gpsimd.tensor_copy(out=ident_bf[:], in_=ident[:])
        half_b_gate = keep.tile([P, SLOTS], F32, name="half_b_gate")
        nc.gpsimd.tensor_scalar(
            out=half_b_gate[:], in0=b_gate_bf[:], scalar1=0.5, scalar2=0.0, op0=ALU.mult, op1=ALU.add
        )

        x_grouped = keep.tile([P, TOKENS, SLOTS], BF16, name="x_grouped", align_bytes=64)
        x_codes = keep.tile([P, TOKENS], U32, name="x_codes", align_bytes=64)
        x_scales = keep.tile([P, TOKENS], U8, name="x_scales", align_bytes=64)
        wr_grouped = [keep.tile([P, P, SLOTS], BF16, name="wr_grouped%d" % s, align_bytes=64) for s in range(SLOTS)]
        wr_codes = keep.tile([P, H], U32, name="wr_codes", align_bytes=64)
        wr_scales = keep.tile([P, H], U8, name="wr_scales", align_bytes=64)
        wg_parts = [(u, g) for u in range(2) for g in range(2)]
        wg_grouped = {
            part: keep.tile([P, HALF, SLOTS], BF16, name="wg_grouped%d%d" % part, align_bytes=64) for part in wg_parts
        }
        wg_codes = [keep.tile([P, H], U32, name="wg_codes%d" % g, align_bytes=64) for g in range(2)]
        wg_scales = [keep.tile([P, H], U8, name="wg_scales%d" % g, align_bytes=64) for g in range(2)]
        projected = [keep.tile([P, SLOTS, P], F32, name="projected%d" % n) for n in range(TOKEN_TILES)]
        r_grouped = [keep.tile([P, P, SLOTS], BF16, name="r_grouped%d" % n, align_bytes=64) for n in range(TOKEN_TILES)]
        r_codes = keep.tile([P, TOKENS], U32, name="r_codes", align_bytes=64)
        r_scales = keep.tile([P, TOKENS], U8, name="r_scales", align_bytes=64)
        diff = [keep.tile([P, SLOTS, P], F32, name="diff%d" % n) for n in range(TOKEN_TILES)]

        def tokens_of(n):
            return slice(n * P, (n + 1) * P)

        def half_cols(u):
            return slice(u * HALF, (u + 1) * HALF)

        b_route_t = psum.tile([P, SLOTS, P], BF16, tag="bank", name="b_route_t")
        for s in range(SLOTS):
            nc.tensor.transpose(b_route_t[:, s, :], b_route_bf[:, s : s + 1].to_broadcast([P, P]), ident_bf[:])
        b_route_rows = keep.tile([P, SLOTS, P], BF16, name="b_route_rows")
        nc.scalar.copy(out=b_route_rows[:], in_=b_route_t[:])
        x_words = psum.tile([P, 2, HALF], F32, tag="bank", name="x_words")
        wr_words = [psum.tile([P, 2, P], F32, tag="bank", name="wr_words") for s in range(SLOTS)]
        routing_ps = psum.tile([P, BANK], F32, tag="bank", name="routing_ps")
        angles_thr = routing_ps[:, 0 : WIDTH + 1]
        angles = routing_ps[:, 0:WIDTH]
        sums = routing_ps[:, 2 * WIDTH : 2 * WIDTH + LIMBS]
        nc.tensor.matmul(
            out=angles_thr, lhsT=small_col[:, 0:1].to_broadcast([P, P]), rhs=of_limb[:], start=True, stop=False
        )
        nc.tensor.matmul(
            out=angles_thr, lhsT=small_own[:].rearrange("k a j -> k (a j)"), rhs=of_own[:], start=False, stop=True
        )
        transpose_words(nc, x_words, ident[:], [x_sb[:, n, :] for n in range(TOKEN_TILES)])
        TURN = 1.0 / (4.0 * math.pi)
        turns = keep.tile([P, WIDTH], F32, name="turns")
        nc.vector.tensor_scalar(out=turns[:], in0=angles, scalar1=TURN, scalar2=None, op0=ALU.mult)
        rounded = keep.tile([P, WIDTH], F32, name="rounded")
        nc.vector.tensor_scalar(
            out=rounded[:], in0=angles, scalar1=TURN, scalar2=ROUND_MAGIC, op0=ALU.mult, op1=ALU.add
        )
        minus_frac = keep.tile([P, WIDTH], F32, name="minus_frac")
        nc.vector.scalar_tensor_tensor(
            out=minus_frac[:], in0=rounded[:], scalar=ROUND_MAGIC, in1=turns[:], op0=ALU.subtract, op1=ALU.subtract
        )
        minus_thr = keep.tile([P, 1], F32, name="minus_thr")
        nc.vector.tensor_copy(out=minus_thr[:], in_=routing_ps[:, WIDTH : WIDTH + 1])
        for s in range(SLOTS):
            transpose_words(nc, wr_words[s], ident[:], [wr_sb[:, s, :]])

        def quantise_wr(s):
            quantise(nc, wr_grouped[s][:], wr_codes[:, s * P : (s + 1) * P], wr_scales[:, s * P : (s + 1) * P])

        sines = keep.tile([P, WIDTH], F32, name="sines")
        nc.scalar.activation(out=sines[:], in_=minus_frac[:], func=ACT.Sin, scale=-2.0 * math.pi)
        group_words(nc.vector.tensor_copy, x_words[:], x_grouped[:])
        group_words(nc.scalar.copy, wr_words[0][:], wr_grouped[0][:])
        gyroid = keep.tile([P, LIMBS], F32, name="gyroid")
        nc.vector.tensor_reduce(
            out=gyroid[:], in_=sines[:].rearrange("p (w i) -> p i w", i=LIMBS), axis=AXIS_X, op=ALU.add
        )
        quantise(nc, x_grouped[:], x_codes[:], x_scales[:])
        group_words(nc.scalar.copy, wr_words[1][:], wr_grouped[1][:])
        tanh_f = keep.tile([P, LIMBS], F32, name="tanh_f")
        nc.scalar.activation(out=tanh_f[:], in_=gyroid[:], func=ACT.Tanh, scale=0.5, bias=minus_thr[:, 0:1])
        for s in range(2, SLOTS):
            group_words(nc.scalar.copy, wr_words[s][:], wr_grouped[s][:])
        for s in range(2):
            quantise_wr(s)
        twice_r_eps = keep.tile([P, LIMBS], F32, name="twice_r_eps")
        nc.vector.scalar_tensor_tensor(
            out=twice_r_eps[:], in0=tanh_f[:], scalar=1.0, in1=diag_and_eps[:], op0=ALU.add, op1=ALU.max
        )
        twice_r = keep.tile([P, LIMBS], F32, name="twice_r")
        nc.vector.scalar_tensor_tensor(
            out=twice_r[:], in0=tanh_f[:], scalar=1.0, in1=two_on_diag[:], op0=ALU.add, op1=ALU.max
        )
        quantise_wr(2)
        quantise_wr(3)
        twice_mixer = keep.tile([P, GROUPS, LIMBS], F32, name="twice_mixer")
        nc.vector.tensor_tensor(
            out=twice_mixer[:],
            in0=own_group[:].unsqueeze(2).to_broadcast([P, GROUPS, LIMBS]),
            in1=twice_r[:].unsqueeze(1).to_broadcast([P, GROUPS, LIMBS]),
            op=ALU.mult,
        )

        def transpose_w_gate(words, u, g):
            transpose_words(nc, words, ident[:], [wg_sb[:, 2 * u + e, g * H : (g + 1) * H] for e in range(2)])

        def group_w_gate(copy, words, u, g):
            group_words(copy, words[:], wg_grouped[(u, g)][:])

        first_words = [psum.tile([P, 2, HALF], F32, tag="bank", name="wg_words") for part in wg_parts[:2]]
        for words, part in zip(first_words, wg_parts):
            transpose_w_gate(words, *part)
            group_w_gate(nc.scalar.copy, words, *part)
        x_twice = keep.tile([P, SLOTS, P], F32, name="x_twice")
        nc.scalar.activation(
            out=x_twice[:], in_=x_grouped[:, tokens_of(0), :].rearrange("q t s -> q s t"), func=ACT.Copy, scale=2.0
        )

        def project(u):
            for n in range(TOKEN_TILES):
                nc.tensor.matmul_mx(
                    out=proj_ps[(n, u)][:],
                    lhsT=x_codes[:, tokens_of(n)].bitcast(FP8X4),
                    lhsT_scale=x_scales[:, tokens_of(n)],
                    rhs=wr_codes[:, half_cols(u)].bitcast(FP8X4),
                    rhs_scale=wr_scales[:, half_cols(u)],
                    start=True,
                    stop=True,
                )

        proj_ps = {
            (n, u): psum.tile([P, HALF], F32, tag="bank", name="proj_ps") for u in range(2) for n in range(TOKEN_TILES)
        }
        late_words = [psum.tile([P, 2, HALF], F32, tag="bank", name="wg_words") for part in wg_parts[2:]]
        def add_b_route(n, u):
            nc.vector.tensor_tensor(
                out=projected[n][:, 2 * u : 2 * u + 2, :].rearrange("t s q -> t (s q)"),
                in0=proj_ps[(n, u)][:],
                in1=b_route_rows[:, 2 * u : 2 * u + 2, :].rearrange("t s q -> t (s q)"),
                op=ALU.add,
            )

        nc.tensor.matmul(
            out=sums, lhsT=sixteenth[:, 0:1].to_broadcast([P, P]), rhs=twice_r_eps[:], start=True, stop=True
        )
        project(0)
        project(1)
        row_inv = keep.tile([P, LIMBS], F32, name="row_inv")
        nc.vector.reciprocal(out=row_inv[:], in_=sums)
        add_b_route(0, 0)
        mixer = keep.tile([P, GROUPS, LIMBS], F32, name="mixer")
        nc.vector.tensor_tensor(
            out=mixer[:],
            in0=twice_mixer[:],
            in1=row_inv[:].unsqueeze(1).to_broadcast([P, GROUPS, LIMBS]),
            op=ALU.mult,
        )
        add_b_route(0, 1)
        add_b_route(1, 0)
        add_b_route(1, 1)
        for words, part in zip(late_words, wg_parts[2:]):
            transpose_w_gate(words, *part)
            group_w_gate(nc.scalar.copy, words, *part)

        routed_ps = {
            (n, u): psum.tile([P, 2, P], F32, tag="bank", name="routed_ps") for n in range(TOKEN_TILES) for u in range(2)
        }

        def mix(n, u):
            for e in range(2):
                nc.tensor.matmul(
                    out=routed_ps[(n, u)][:, e, :],
                    lhsT=projected[n][:, 2 * u + e, :],
                    rhs=mixer[:].rearrange("t a i -> t (a i)"),
                    start=True,
                    stop=True,
                )

        def round_routed(n, u):
            nc.scalar.copy(
                out=r_grouped[n][:, :, 2 * u : 2 * u + 2], in_=routed_ps[(n, u)][:].rearrange("q e t -> q t e")
            )

        def quantise_routed(n):
            quantise(nc, r_grouped[n][:], r_codes[:, tokens_of(n)], r_scales[:, tokens_of(n)])

        def subtract_x(n, u):
            slots = slice(2 * u, 2 * u + 2)
            nc.vector.tensor_tensor(
                out=diff[n][:, slots, :],
                in0=routed_ps[(n, u)][:],
                in1=x_grouped[:, tokens_of(n), slots].rearrange("q t e -> q e t"),
                op=ALU.subtract,
            )

        def quantise_w_gate(u, g):
            quantise(nc, wg_grouped[(u, g)][:], wg_codes[g][:, half_cols(u)], wg_scales[g][:, half_cols(u)])

        for u in range(2):
            mix(0, u)
            round_routed(0, u)
        for u in range(2):
            mix(1, u)
            round_routed(1, u)
        for part in wg_parts:
            quantise_w_gate(*part)
        subtract_x(0, 0)
        quantise_routed(0)
        subtract_x(0, 1)

        def gate_pass(out, n, s, g):
            feats = slice(s * P, (s + 1) * P)
            codes, scales = ((x_codes, x_scales), (r_codes, r_scales))[g]
            nc.tensor.matmul_mx(
                out=out,
                lhsT=wg_codes[g][:, feats].bitcast(FP8X4),
                lhsT_scale=wg_scales[g][:, feats],
                rhs=codes[:, tokens_of(n)].bitcast(FP8X4),
                rhs_scale=scales[:, tokens_of(n)],
                start=(g == 0),
                stop=(g == 1),
            )

        tanh_g = [keep.tile([P, SLOTS, P], F32, name="tanh_g%d" % n) for n in range(TOKEN_TILES)]

        def gate(out, n, s):
            nc.scalar.activation(
                out=tanh_g[n][:, s, :], in_=out, func=ACT.Tanh, scale=0.5, bias=half_b_gate[:, s : s + 1]
            )

        gates_0 = [psum.tile([P, 2, P], F32, tag="bank", name="gates_0") for u in range(2)]
        for s in range(SLOTS):
            for g in range(2):
                gate_pass(gates_0[s // 2][:, s % 2, :], 0, s, g)
        gates_1 = [psum.tile([P, P], F32, tag="bank", name="gates_1") for s in range(SLOTS)]
        for s in range(SLOTS):
            gate_pass(gates_1[s][:], 1, s, 0)
        subtract_x(1, 0)
        quantise_routed(1)
        subtract_x(1, 1)
        for s in range(SLOTS):
            gate_pass(gates_1[s][:], 1, s, 1)
        for s in range(SLOTS):
            gate(gates_0[s // 2][:, s % 2, :], 0, s)
        for s in range(SLOTS):
            gate(gates_1[s][:], 1, s)

        moved = [keep.tile([P, SLOTS, P], F32, name="moved%d" % n) for n in range(TOKEN_TILES)]

        def weigh(n, slots):
            nc.vector.scalar_tensor_tensor(
                out=moved[n][:, slots, :].rearrange("q e t -> q (e t)"),
                in0=tanh_g[n][:, slots, :].rearrange("q e t -> q (e t)"),
                scalar=1.0,
                in1=diff[n][:, slots, :].rearrange("q e t -> q (e t)"),
                op0=ALU.add,
                op1=ALU.mult,
            )

        def transpose_back(moved_t, tile, slots, start, stop):
            for s in slots:
                nc.tensor.matmul(
                    out=moved_t[:, s, :],
                    lhsT=tile[:, s, :],
                    rhs=ident[:],
                    start=start and s == slots[0],
                    stop=stop and s == slots[-1],
                    is_transpose=True,
                )

        def add_x_and_store(moved_t, n, h):
            feats = half_cols(h)
            out_sb = keep.tile([P, HALF], F32, name="out_sb%d%d" % (n, h))
            nc.vector.scalar_tensor_tensor(
                out=out_sb[:].rearrange("t (q s) -> t q s", s=SLOTS),
                in0=moved_t[:, :, h * (P // 2) : (h + 1) * (P // 2)].rearrange("t s q -> t q s"),
                scalar=0.5,
                in1=x_sb[:, n, feats].rearrange("t (q s) -> t q s", s=SLOTS),
                op0=ALU.mult,
                op1=ALU.add,
            )
            nc.sync.dma_start(out=out_rows[tokens_of(n), feats], in_=out_sb[:])

        moved_t = [psum.tile([P, SLOTS, P], F32, tag="bank", name="moved_t%d" % n) for n in range(TOKEN_TILES)]
        transpose_back(moved_t[0], x_twice, (0, 1, 2, 3), True, False)
        weigh(0, slice(0, 2))
        transpose_back(moved_t[0], moved[0], (0, 1), False, False)
        weigh(0, slice(2, 4))
        transpose_back(moved_t[0], moved[0], (2, 3), False, True)
        out_0 = keep.tile([P, H], F32, name="out_0")
        for h in range(2):
            nc.scalar.activation(
                out=out_0[:, half_cols(h)].rearrange("t (q s) -> t q s", s=SLOTS),
                in_=moved_t[0][:, :, h * (P // 2) : (h + 1) * (P // 2)].rearrange("t s q -> t q s"),
                func=ACT.Copy,
                scale=0.5,
            )
            nc.sync.dma_start(out=out_rows[tokens_of(0), half_cols(h)], in_=out_0[:, half_cols(h)])
        for s in range(SLOTS):
            weigh(1, slice(s, s + 1))
            nc.tensor.transpose(moved_t[1][:, s, :], moved[1][:, s, :], ident[:])
        for h in range(2):
            add_x_and_store(moved_t[1], 1, h)
